import numpy as np
import ml_dtypes


def mxq(x, axis, fmt="e4m3"):
    dtype, down = {"e4m3": (ml_dtypes.float8_e4m3fn, 7), "e5m2": (ml_dtypes.float8_e5m2, 14)}[fmt]
    v = np.moveaxis(np.asarray(x, np.float32).astype(ml_dtypes.bfloat16).astype(np.float64), axis, -1)
    blocks = v.reshape(v.shape[:-1] + (-1, 32))
    amax = np.abs(blocks).max(-1, keepdims=True)
    byte = np.maximum(np.where(amax > 0, np.frexp(amax)[1] - 1 + 127, 0) - down, 1)
    scale = np.exp2(byte - 127.0)
    codes = (blocks / scale).astype(np.float32).astype(dtype).astype(np.float64)
    return np.moveaxis((codes * scale).reshape(v.shape), -1, axis)


WIDE = False


def mx_kscale(k):
    if not WIDE:
        return np.ones(k)
    levels = np.array([10, -10, 5, -5, 0])
    a = np.random.permutation(np.resize(levels, k // 512 * 4)).reshape(k // 512, 4)
    idx = np.arange(k)
    return np.exp2(a[idx // 512, idx % 128 // 32])


BF16 = ml_dtypes.bfloat16


def bf(x):
    return np.asarray(x, np.float32).astype(BF16)


def f64(x):
    return np.asarray(x).astype(np.float64)


E2M1 = np.array([0.0, 0.5, 1.0, 1.5, 2.0, 3.0, 4.0, 6.0, -0.0, -0.5, -1.0, -1.5, -2.0, -3.0, -4.0, -6.0])


def pack_weight(w, fmt):
    k, n = w.shape
    w = f64(bf(w)).reshape(k // 32, 32, n)
    amax = np.abs(w).max(1)
    if fmt == "e4m3":
        byte = np.frexp(amax)[1] - 1 + 127 - 7
    else:
        mant, ex = np.frexp(amax / 6.0)
        byte = np.where(mant > 0.5, ex, ex - 1) + 127
    byte = np.clip(np.where(amax > 0, byte, 1), 1, 254)
    scaled = (w * np.exp2(127.0 - byte)[:, None, :]).reshape(k, n).astype(np.float32)
    by_word = np.ascontiguousarray(scaled.reshape(k // 512, 128, 4, n).transpose(0, 1, 3, 2))
    if fmt == "e4m3":
        words = by_word.astype(ml_dtypes.float8_e4m3fn).view(np.uint8)
    else:
        c = by_word.astype(ml_dtypes.float4_e2m1fn).view(np.uint8) & 0xF
        words = c[..., 0::2] | (c[..., 1::2] << 4)
    return np.ascontiguousarray(words), np.ascontiguousarray(byte.astype(np.uint8).reshape(k // 512, 16, n))


def unpack_weight(words, scales, fmt):
    g, p, n, _ = words.shape
    if fmt == "e4m3":
        vals = np.ascontiguousarray(words).view(ml_dtypes.float8_e4m3fn).astype(np.float64)
    else:
        nib = np.empty((g, p, n, 4), np.uint8)
        nib[..., 0::2] = words & 0xF
        nib[..., 1::2] = words >> 4
        vals = E2M1[nib]
    vals = vals * np.repeat(np.exp2(scales.astype(np.float64) - 127.0), 8, axis=1)[..., None]
    return vals.transpose(0, 1, 3, 2).reshape(g * 512, n)

def pack4(w):
    words, scales = pack_weight(w, "e2m1")
    return words.reshape(words.shape[0], 128, -1), scales


def unpack4(words, scales):
    return unpack_weight(words.reshape(words.shape[0], 128, -1, 2), scales, "e2m1")


B, D, H, K = 512, 1024, 16384, 128
EPS_B = 1e-8


def silu(v):
    return v / (1.0 + np.exp(-v))


def softplus(v):
    return np.maximum(v, 0.0) + np.log(1.0 + np.exp(-np.abs(v)))


def setup_inputs():
    s = mx_kscale(H)
    h_act = bf(silu(np.random.standard_normal((B, H))) * s)
    W3_words, W3_scales = pack4(np.random.standard_normal((H, K)) * 3.0 / np.sqrt(H) / s[:, None])
    b3 = bf(0.5 * np.random.standard_normal(K))
    return {"h_act": h_act,
            "W3_words": W3_words,
            "W3_scales": W3_scales,
            "b3": b3}


def reference(h_act, W3_words, W3_scales, b3):
    logits = (mxq(f64(h_act), 1, "e4m3") @ unpack4(W3_words, W3_scales)) + f64(b3)
    evidence = softplus(logits)
    alpha = evidence + 1.0
    S = alpha.sum(-1, keepdims=True)
    expected_prob = alpha / S
    vacuity = float(K) / S[:, 0]
    belief = evidence / S
    full = np.zeros(belief.shape[0])
    for i in range(K):
        bi = belief[:, i:i + 1]
        full = full + ((1.0 - np.abs(bi - belief) / (bi + belief + EPS_B)) * bi * belief).sum(-1)
    dissonance = 0.5 * (full - (belief * belief).sum(-1))
    return (alpha, evidence, expected_prob, vacuity, dissonance)

@@ -1,0 +1,386 @@
+from contextlib import ExitStack
+
+import concourse.mybir as mybir
+from concourse.masks import make_identity
+
+F32 = mybir.dt.float32
+BF16 = mybir.dt.bfloat16
+I32 = mybir.dt.int32
+U8 = mybir.dt.uint8
+U32 = mybir.dt.uint32
+FP8X4 = mybir.dt.float8_e4m3fn_x4
+FP4X4 = mybir.dt.float4_e2m1fn_x4
+ACT = mybir.ActivationFunctionType
+ALU = mybir.AluOpType
+AX = mybir.AxisListType
+
+P = 128
+ROWS = 512
+K_DIM = 16384
+C = 128
+EPS_B = 1e-8
+FLOPS = 2 * ROWS * K_DIM * C
+
+BLOCKS = ROWS // P
+K_PASS = 4 * P
+GROUPS = K_DIM // K_PASS
+PAIRS_PER_GROUP = K_PASS // 2
+
+STEP_GROUPS = 8
+STEP_K = STEP_GROUPS * K_PASS
+STEPS_PER_BLOCK = GROUPS // STEP_GROUPS
+STEPS = BLOCKS * STEPS_PER_BLOCK
+BANK_GROUPS = 2
+STEP_BANKS = STEP_GROUPS // BANK_GROUPS
+BANKS = STEPS * STEP_BANKS
+BANKS_AHEAD = 6
+H_BUFS = 8
+
+HALF = C // 2
+CHUNK_I = 32
+CHUNKS_PER_BLOCK = C // CHUNK_I
+CHUNKS = BLOCKS * CHUNKS_PER_BLOCK
+FE_STEPS_PER_CHUNK = 4
+
+
+def tile_evidentialhead_pb_k_kernel(
+    tc, h_act, W3_words, W3_scales, b3, out_0, out_1, out_2, out_3, out_4
+):
+    nc = tc.nc
+    h_rows = h_act.rearrange("(b p) k -> p b k", p=P)
+
+    with ExitStack() as stack:
+        const = stack.enter_context(tc.tile_pool(name="const", bufs=1))
+        h_pool = stack.enter_context(tc.tile_pool(name="h", bufs=H_BUFS))
+        grouped_pool = stack.enter_context(tc.tile_pool(name="grouped", bufs=2))
+        codes_pool = stack.enter_context(tc.tile_pool(name="codes", bufs=2))
+        pair_pool = stack.enter_context(tc.tile_pool(name="pair", bufs=3))
+        psum_t = stack.enter_context(tc.psum_pool(name="psum_t", bufs=BANKS_AHEAD))
+        psum_acc = stack.enter_context(tc.psum_pool(name="psum_acc", bufs=1))
+        stack.enter_context(tc.manual_schedule())
+
+        ident = const.tile([P, P], F32, name="ident")
+        w_words = const.tile([P, GROUPS, 2 * C], U8, name="w_words", align_bytes=64)
+        w_planes = const.tile([P, GROUPS, C], U8, name="w_planes", align_bytes=64)
+        b3_all = const.tile([P, C], BF16, name="b3_all")
+
+        logits = const.tile([P, BLOCKS, C], F32, name="logits")
+        neg_abs = const.tile([P, BLOCKS, C], F32, name="neg_abs")
+        decay = const.tile([P, BLOCKS, C], F32, name="decay")
+        log_term = const.tile([P, BLOCKS, C], F32, name="log_term")
+        evidence = const.tile([P, BLOCKS, C], F32, name="evidence")
+        alpha = const.tile([P, BLOCKS, C], F32, name="alpha")
+        prob = const.tile([P, BLOCKS, C], F32, name="prob")
+        squares = const.tile([P, BLOCKS, C], F32, name="squares")
+        log2x = const.tile([P, BLOCKS, 2, C], F32, name="log2x")
+        belief2 = const.tile([P, BLOCKS, 2, C], F32, name="belief2")
+        neg_half_log = const.tile([P, BLOCKS, C], F32, name="neg_half_log")
+        sum_e = const.tile([P, BLOCKS], F32, name="sum_e")
+        half_eps = const.tile([P, BLOCKS], F32, name="half_eps")
+        strength = const.tile([P, BLOCKS], F32, name="strength")
+        inv_s = const.tile([P, BLOCKS], F32, name="inv_s")
+        sum_b = const.tile([P, BLOCKS], F32, name="sum_b")
+        sum_sq = const.tile([P, BLOCKS], F32, name="sum_sq")
+        sq_of_sum = const.tile([P, BLOCKS], F32, name="sq_of_sum")
+        twice_all = const.tile([P, BLOCKS], F32, name="twice_all")
+        part = const.tile([P, 2, BLOCKS, CHUNKS_PER_BLOCK // 2], F32, name="part")
+        total = const.tile([P, BLOCKS], F32, name="total")
+        per_row = const.tile([P, P], F32, name="per_row")
+        per_row_t = const.tile([P, P], F32, name="per_row_t")
+
+        chunks = {}
+        banks = {}
+        grouped_tiles = {}
+        code_tiles = {}
+        acc_tiles = {}
+        tanh_tiles = {}
+        term_tiles = {}
+
+        def load_chunk(f):
+            b, q = divmod(f, STEPS_PER_BLOCK)
+            h_chunk = h_pool.tile([P, STEP_K], BF16, name="h_chunk")
+            nc.sync.dma_start(out=h_chunk[:], in_=h_rows[:, b, q * STEP_K : (q + 1) * STEP_K])
+            chunks[f] = h_chunk
+
+        def load_weights():
+            scale_words = W3_scales.bitcast(I32)
+            for first in range(8):
+                part0 = 32 * (first // 4) + first % 4
+                nc.sync.dma_start(
+                    out=w_planes[part0:P:64, :, :].bitcast(I32),
+                    in_=scale_words[:, first:16:8, :].rearrange("g q n -> q g n"),
+                )
+            nc.sync.dma_start(
+                out=w_words[:].bitcast(I32),
+                in_=W3_words.bitcast(I32).rearrange("g p n -> p g n"),
+            )
+
+        def transpose_bank(n):
+            f, j = divmod(n, STEP_BANKS)
+            pairs = chunks[f][:].bitcast(F32)
+            xt = psum_t.tile([P, BANK_GROUPS, 2, P], F32, name="xt")
+            for g in range(BANK_GROUPS):
+                first = (j * BANK_GROUPS + g) * PAIRS_PER_GROUP
+                for u in range(2):
+                    nc.tensor.transpose(
+                        xt[:, g, u, :],
+                        pairs[:, first + u : first + PAIRS_PER_GROUP : 2],
+                        ident[:],
+                    )
+            banks[n] = xt
+
+        def evacuate_step(f, refill_end=BANKS):
+            grouped = grouped_pool.tile([P, STEP_K], BF16, name="grouped", align_bytes=64)
+            grouped_tiles[f] = grouped
+            dst = grouped[:].bitcast(F32).rearrange(
+                "p (j g r u) -> p j g r u", j=STEP_BANKS, g=BANK_GROUPS, u=2
+            )
+            for j in range(STEP_BANKS):
+                n = f * STEP_BANKS + j
+                src = banks[n][:].rearrange("p g u r -> p g r u")
+                if j == STEP_BANKS - 1:
+                    nc.vector.tensor_copy(out=dst[:, j], in_=src)
+                else:
+                    nc.scalar.copy(out=dst[:, j], in_=src)
+                if n + BANKS_AHEAD < refill_end:
+                    transpose_bank(n + BANKS_AHEAD)
+            if f + H_BUFS < STEPS:
+                load_chunk(f + H_BUFS)
+
+        def quantise_step(f):
+            b, q = divmod(f, STEPS_PER_BLOCK)
+            if q == 0:
+                h_codes = codes_pool.tile([P, GROUPS * P], U32, name="h_codes", align_bytes=64)
+                h_scales = codes_pool.tile([P, GROUPS * P], U8, name="h_scales", align_bytes=64)
+                code_tiles[b] = (h_codes, h_scales)
+            h_codes, h_scales = code_tiles[b]
+            cols = slice(q * STEP_GROUPS * P, (q + 1) * STEP_GROUPS * P)
+            nc.vector.quantize_mx(
+                out=h_codes[:, cols].bitcast(FP8X4),
+                scales=h_scales[:, cols],
+                in_=grouped_tiles[f][:],
+            )
+            if q == STEPS_PER_BLOCK - 1:
+                mx_block(b)
+
+        def mx_block(b):
+            if b == 0:
+                acc_first = psum_acc.tile([P, 1, C], F32, name="acc_first")
+                acc_tiles[0] = acc_first
+            if b == 1:
+                acc_rest = psum_acc.tile([P, BLOCKS - 1, C], F32, name="acc_rest")
+                acc_tiles[1] = acc_rest
+            acc = acc_tiles[0][:, 0, :] if b == 0 else acc_tiles[1][:, b - 1, :]
+            h_codes, h_scales = code_tiles[b]
+            for g in range(GROUPS):
+                rows = slice(g * P, (g + 1) * P)
+                nc.tensor.matmul_mx(
+                    out=acc,
+                    lhsT=h_codes[:, rows].bitcast(FP8X4),
+                    lhsT_scale=h_scales[:, rows],
+                    rhs=w_words[:, g, :].bitcast(FP4X4),
+                    rhs_scale=w_planes[:, g, :],
+                    start=(g == 0),
+                    stop=(g == GROUPS - 1),
+                )
+
+        def head_softplus(b0, b1, acc):
+            blk = slice(b0, b1)
+            nc.vector.tensor_tensor(
+                out=logits[:, blk, :],
+                in0=acc[:],
+                in1=b3_all[:].unsqueeze(1).to_broadcast([P, b1 - b0, C]),
+                op=ALU.add,
+            )
+            nc.vector.scalar_tensor_tensor(
+                out=neg_abs[:, blk, :], in0=logits[:, blk, :], scalar=-1.0,
+                in1=logits[:, blk, :], op0=ALU.mult, op1=ALU.min,
+            )
+            nc.scalar.activation(out=decay[:, blk, :], in_=neg_abs[:, blk, :], func=ACT.Exp)
+            nc.scalar.activation(
+                out=log_term[:, blk, :], in_=decay[:, blk, :], func=ACT.Ln, bias=1.0
+            )
+
+        def head_evidence(b0, b1):
+            blk = slice(b0, b1)
+            nc.vector.scalar_tensor_tensor(
+                out=evidence[:, blk, :], in0=logits[:, blk, :], scalar=0.0,
+                in1=log_term[:, blk, :], op0=ALU.max, op1=ALU.add,
+            )
+            nc.vector.tensor_reduce(
+                out=sum_e[:, blk], in_=evidence[:, blk, :], axis=AX.X, op=ALU.add
+            )
+            nc.vector.tensor_scalar(
+                out=half_eps[:, blk], in0=sum_e[:, blk], scalar1=float(C),
+                scalar2=0.5 * EPS_B, op0=ALU.add, op1=ALU.mult,
+            )
+            for b in range(b0, b1):
+                nc.scalar.activation(
+                    out=log2x[:, b, :, :],
+                    in_=evidence[:, b, :].unsqueeze(1).to_broadcast([P, 2, C]),
+                    func=ACT.Ln,
+                    bias=half_eps[:, b : b + 1],
+                )
+
+        def head_pair_operands(b0, b1):
+            blk = slice(b0, b1)
+            nc.vector.tensor_scalar_mul(
+                out=neg_half_log[:, blk, :], in0=log2x[:, blk, 0, :], scalar1=-0.5
+            )
+            nc.vector.tensor_scalar_add(out=strength[:, blk], in0=sum_e[:, blk], scalar1=float(C))
+            nc.vector.reciprocal(out=inv_s[:, blk], in_=strength[:, blk])
+            for b in range(b0, b1):
+                nc.vector.tensor_scalar_mul(
+                    out=belief2[:, b, :, :],
+                    in0=evidence[:, b, :].unsqueeze(1).to_broadcast([P, 2, C]),
+                    scalar1=inv_s[:, b : b + 1],
+                )
+
+        def head_outputs(b0, b1):
+            blk = slice(b0, b1)
+            nc.vector.tensor_scalar_add(out=alpha[:, blk, :], in0=evidence[:, blk, :], scalar1=1.0)
+            for b in range(b0, b1):
+                nc.vector.tensor_scalar_mul(
+                    out=prob[:, b, :], in0=alpha[:, b, :], scalar1=inv_s[:, b : b + 1]
+                )
+            nc.vector.tensor_scalar_mul(out=per_row[:, blk], in0=inv_s[:, blk], scalar1=float(C))
+            nc.vector.tensor_tensor(
+                out=squares[:, blk, :], in0=belief2[:, blk, 0, :], in1=belief2[:, blk, 0, :],
+                op=ALU.mult,
+            )
+            nc.vector.tensor_reduce(
+                out=sum_sq[:, blk], in_=squares[:, blk, :], axis=AX.X, op=ALU.add
+            )
+            nc.vector.tensor_tensor(
+                out=sum_b[:, blk], in0=sum_e[:, blk], in1=inv_s[:, blk], op=ALU.mult
+            )
+            nc.vector.tensor_tensor(
+                out=sq_of_sum[:, blk], in0=sum_b[:, blk], in1=sum_b[:, blk], op=ALU.mult
+            )
+            nc.vector.tensor_tensor(
+                out=twice_all[:, blk], in0=sq_of_sum[:, blk], in1=sum_sq[:, blk], op=ALU.subtract
+            )
+
+        def run_length(c):
+            return HALF if c * CHUNK_I < HALF else HALF - 1
+
+        def tanh_chunk(k):
+            b, c = divmod(k, CHUNKS_PER_BLOCK)
+            n = run_length(c)
+            logs = log2x[:, b, :, :].rearrange("p d c -> p (d c)")
+            tanh_t = pair_pool.tile([P, CHUNK_I, HALF], F32, name="tanh_t")
+            tanh_tiles[k] = tanh_t
+            for ii in range(CHUNK_I):
+                i = c * CHUNK_I + ii
+                nc.scalar.activation(
+                    out=tanh_t[:, ii, :n],
+                    in_=logs[:, i + 1 : i + 1 + n],
+                    func=ACT.Tanh,
+                    scale=0.5,
+                    bias=neg_half_log[:, b, i : i + 1],
+                )
+
+        def weight_chunk(k):
+            b, c = divmod(k, CHUNKS_PER_BLOCK)
+            n = run_length(c)
+            beliefs = belief2[:, b, :, :].rearrange("p d c -> p (d c)")
+            tanh_t = tanh_tiles[k]
+            term = pair_pool.tile([P, CHUNK_I, HALF], F32, name="term")
+            term_tiles[k] = term
+            for ii in range(CHUNK_I):
+                i = c * CHUNK_I + ii
+                nc.vector.scalar_tensor_tensor(
+                    out=term[:, ii, :n],
+                    in0=tanh_t[:, ii, :n],
+                    scalar=beliefs[:, i : i + 1],
+                    in1=beliefs[:, i + 1 : i + 1 + n],
+                    op0=ALU.mult,
+                    op1=ALU.mult,
+                )
+
+        def abs_sum(k):
+            b, c = divmod(k, CHUNKS_PER_BLOCK)
+            n = run_length(c)
+            term = term_tiles[k]
+            if k % 2 == 0:
+                nc.scalar.activation(
+                    out=term[:, :, :n], in_=term[:, :, :n], func=ACT.Abs,
+                    accum_out=part[:, 0, b, c // 2 : c // 2 + 1],
+                )
+            else:
+                nc.vector.scalar_tensor_tensor(
+                    out=term[:, :, :n], in0=term[:, :, :n], scalar=-1.0, in1=term[:, :, :n],
+                    op0=ALU.mult, op1=ALU.max,
+                    accum_out=part[:, 1, b, c // 2 : c // 2 + 1],
+                )
+
+        nc.vector.memset(w_planes[:].bitcast(I32), 0)
+        make_identity(nc, ident[:])
+        nc.gpsimd.memset(per_row[:], 0.0)
+        nc.scalar.dma_start(out=b3_all[:], in_=b3.partition_broadcast(P))
+        for f in range(STEPS_PER_BLOCK):
+            load_chunk(f)
+        load_weights()
+        for f in range(STEPS_PER_BLOCK, H_BUFS):
+            load_chunk(f)
+        for n in range(BANKS_AHEAD):
+            transpose_bank(n)
+
+        block_banks = STEPS_PER_BLOCK * STEP_BANKS
+        for f in range(STEPS_PER_BLOCK):
+            evacuate_step(f, refill_end=block_banks)
+            quantise_step(f)
+        for n in range(block_banks, block_banks + BANKS_AHEAD):
+            transpose_bank(n)
+        head_softplus(0, 1, acc_tiles[0])
+        evacuate_step(4)
+        head_evidence(0, 1)
+        quantise_step(4)
+        evacuate_step(5)
+        head_pair_operands(0, 1)
+        head_outputs(0, 1)
+
+        first_step = 6
+        for k in range(CHUNKS_PER_BLOCK - 1):
+            tanh_chunk(k)
+            weight_chunk(k)
+            lo = first_step + k * FE_STEPS_PER_CHUNK
+            for f in range(lo, min(lo + FE_STEPS_PER_CHUNK, STEPS)):
+                quantise_step(f - 1)
+                evacuate_step(f)
+            if k > 0:
+                abs_sum(k - 1)
+        quantise_step(STEPS - 1)
+        tanh_chunk(3)
+        weight_chunk(3)
+        abs_sum(2)
+        head_softplus(1, BLOCKS, acc_tiles[1])
+        abs_sum(3)
+        head_evidence(1, BLOCKS)
+        head_pair_operands(1, BLOCKS)
+        head_outputs(1, BLOCKS)
+        nc.sync.dma_start(out=out_0.rearrange("(b p) c -> p b c", p=P), in_=alpha[:])
+        nc.sync.dma_start(out=out_1.rearrange("(b p) c -> p b c", p=P), in_=evidence[:])
+        nc.sync.dma_start(out=out_2.rearrange("(b p) c -> p b c", p=P), in_=prob[:])
+
+        for k in range(CHUNKS_PER_BLOCK, CHUNKS):
+            tanh_chunk(k)
+            weight_chunk(k)
+            if k > CHUNKS_PER_BLOCK:
+                abs_sum(k - 1)
+        abs_sum(CHUNKS - 1)
+
+        nc.vector.tensor_reduce(
+            out=total[:], in_=part[:].rearrange("p e b j -> p b e j"), axis=AX.XY, op=ALU.add
+        )
+        nc.vector.scalar_tensor_tensor(
+            out=per_row[:, BLOCKS : 2 * BLOCKS], in0=twice_all[:], scalar=0.5, in1=total[:],
+            op0=ALU.mult, op1=ALU.subtract,
+        )
+        turned = psum_t.tile([P, P], F32, name="turned", tag="xt")
+        nc.tensor.transpose(turned[:], per_row[:], ident[:])
+        nc.vector.tensor_copy(out=per_row_t[:], in_=turned[:])
+        nc.sync.dma_start(out=out_3.rearrange("(b p) -> b p", p=P), in_=per_row_t[0:BLOCKS, :])
+        nc.sync.dma_start(
+            out=out_4.rearrange("(b p) -> b p", p=P), in_=per_row_t[BLOCKS : 2 * BLOCKS, :]
+        )

@@ -40,7 +40,8 @@ HALF = C // 2
 CHUNK_I = 32
 CHUNKS_PER_BLOCK = C // CHUNK_I
 CHUNKS = BLOCKS * CHUNKS_PER_BLOCK
-FE_STEPS_PER_CHUNK = 4
+FE_LEAD = 6
+W_PIECES = 4
 
 
 def tile_evidentialhead_pb_k_kernel(
@@ -56,7 +57,7 @@ def tile_evidentialhead_pb_k_kernel(
         codes_pool = stack.enter_context(tc.tile_pool(name="codes", bufs=2))
         pair_pool = stack.enter_context(tc.tile_pool(name="pair", bufs=3))
         psum_t = stack.enter_context(tc.psum_pool(name="psum_t", bufs=BANKS_AHEAD))
-        psum_acc = stack.enter_context(tc.psum_pool(name="psum_acc", bufs=1))
+        psum_acc = stack.enter_context(tc.psum_pool(name="psum_acc", bufs=2))
         stack.enter_context(tc.manual_schedule())
 
         ident = const.tile([P, P], F32, name="ident")
@@ -81,7 +82,6 @@ def tile_evidentialhead_pb_k_kernel(
         inv_s = const.tile([P, BLOCKS], F32, name="inv_s")
         sum_b = const.tile([P, BLOCKS], F32, name="sum_b")
         sum_sq = const.tile([P, BLOCKS], F32, name="sum_sq")
-        sq_of_sum = const.tile([P, BLOCKS], F32, name="sq_of_sum")
         twice_all = const.tile([P, BLOCKS], F32, name="twice_all")
         part = const.tile([P, 2, BLOCKS, CHUNKS_PER_BLOCK // 2], F32, name="part")
         total = const.tile([P, BLOCKS], F32, name="total")
@@ -110,10 +110,13 @@ def tile_evidentialhead_pb_k_kernel(
                     out=w_planes[part0:P:64, :, :].bitcast(I32),
                     in_=scale_words[:, first:16:8, :].rearrange("g q n -> q g n"),
                 )
-            nc.sync.dma_start(
-                out=w_words[:].bitcast(I32),
-                in_=W3_words.bitcast(I32).rearrange("g p n -> p g n"),
-            )
+            words = W3_words.bitcast(I32).rearrange("g p n -> p g n")
+            piece = GROUPS // W_PIECES
+            for g0 in range(0, GROUPS, piece):
+                nc.sync.dma_start(
+                    out=w_words[:, g0 : g0 + piece, :].bitcast(I32),
+                    in_=words[:, g0 : g0 + piece, :],
+                )
 
         def transpose_bank(n):
             f, j = divmod(n, STEP_BANKS)
@@ -164,18 +167,13 @@ def tile_evidentialhead_pb_k_kernel(
                 mx_block(b)
 
         def mx_block(b):
-            if b == 0:
-                acc_first = psum_acc.tile([P, 1, C], F32, name="acc_first")
-                acc_tiles[0] = acc_first
-            if b == 1:
-                acc_rest = psum_acc.tile([P, BLOCKS - 1, C], F32, name="acc_rest")
-                acc_tiles[1] = acc_rest
-            acc = acc_tiles[0][:, 0, :] if b == 0 else acc_tiles[1][:, b - 1, :]
+            acc = psum_acc.tile([P, C], F32, name="acc")
+            acc_tiles[b] = acc
             h_codes, h_scales = code_tiles[b]
             for g in range(GROUPS):
                 rows = slice(g * P, (g + 1) * P)
                 nc.tensor.matmul_mx(
-                    out=acc,
+                    out=acc[:],
                     lhsT=h_codes[:, rows].bitcast(FP8X4),
                     lhsT_scale=h_scales[:, rows],
                     rhs=w_words[:, g, :].bitcast(FP4X4),
@@ -184,81 +182,64 @@ def tile_evidentialhead_pb_k_kernel(
                     stop=(g == GROUPS - 1),
                 )
 
-        def head_softplus(b0, b1, acc):
-            blk = slice(b0, b1)
+        def head_logits(b):
             nc.vector.tensor_tensor(
-                out=logits[:, blk, :],
-                in0=acc[:],
-                in1=b3_all[:].unsqueeze(1).to_broadcast([P, b1 - b0, C]),
-                op=ALU.add,
+                out=logits[:, b, :], in0=acc_tiles[b][:], in1=b3_all[:], op=ALU.add
             )
             nc.vector.scalar_tensor_tensor(
-                out=neg_abs[:, blk, :], in0=logits[:, blk, :], scalar=-1.0,
-                in1=logits[:, blk, :], op0=ALU.mult, op1=ALU.min,
-            )
-            nc.scalar.activation(out=decay[:, blk, :], in_=neg_abs[:, blk, :], func=ACT.Exp)
-            nc.scalar.activation(
-                out=log_term[:, blk, :], in_=decay[:, blk, :], func=ACT.Ln, bias=1.0
+                out=neg_abs[:, b, :], in0=logits[:, b, :], scalar=-1.0, in1=logits[:, b, :],
+                op0=ALU.mult, op1=ALU.min,
             )
 
-        def head_evidence(b0, b1):
-            blk = slice(b0, b1)
+        def head_log_term(b):
+            nc.scalar.activation(out=decay[:, b, :], in_=neg_abs[:, b, :], func=ACT.Exp)
+            nc.scalar.activation(out=log_term[:, b, :], in_=decay[:, b, :], func=ACT.Ln, bias=1.0)
+
+        def head_evidence(b):
+            one = slice(b, b + 1)
             nc.vector.scalar_tensor_tensor(
-                out=evidence[:, blk, :], in0=logits[:, blk, :], scalar=0.0,
-                in1=log_term[:, blk, :], op0=ALU.max, op1=ALU.add,
-            )
-            nc.vector.tensor_reduce(
-                out=sum_e[:, blk], in_=evidence[:, blk, :], axis=AX.X, op=ALU.add
+                out=evidence[:, b, :], in0=logits[:, b, :], scalar=0.0, in1=log_term[:, b, :],
+                op0=ALU.max, op1=ALU.add, accum_out=sum_e[:, one],
             )
             nc.vector.tensor_scalar(
-                out=half_eps[:, blk], in0=sum_e[:, blk], scalar1=float(C),
+                out=half_eps[:, one], in0=sum_e[:, one], scalar1=float(C),
                 scalar2=0.5 * EPS_B, op0=ALU.add, op1=ALU.mult,
             )
-            for b in range(b0, b1):
-                nc.scalar.activation(
-                    out=log2x[:, b, :, :],
-                    in_=evidence[:, b, :].unsqueeze(1).to_broadcast([P, 2, C]),
-                    func=ACT.Ln,
-                    bias=half_eps[:, b : b + 1],
-                )
+            nc.scalar.activation(
+                out=log2x[:, b, :, :],
+                in_=evidence[:, b, :].unsqueeze(1).to_broadcast([P, 2, C]),
+                func=ACT.Ln,
+                bias=half_eps[:, one],
+            )
 
-        def head_pair_operands(b0, b1):
-            blk = slice(b0, b1)
+        def head_pair_operands(b):
+            one = slice(b, b + 1)
+            nc.vector.tensor_scalar_add(out=strength[:, one], in0=sum_e[:, one], scalar1=float(C))
+            nc.vector.reciprocal(out=inv_s[:, one], in_=strength[:, one])
             nc.vector.tensor_scalar_mul(
-                out=neg_half_log[:, blk, :], in0=log2x[:, blk, 0, :], scalar1=-0.5
+                out=belief2[:, b, :, :],
+                in0=evidence[:, b, :].unsqueeze(1).to_broadcast([P, 2, C]),
+                scalar1=inv_s[:, one],
             )
-            nc.vector.tensor_scalar_add(out=strength[:, blk], in0=sum_e[:, blk], scalar1=float(C))
-            nc.vector.reciprocal(out=inv_s[:, blk], in_=strength[:, blk])
-            for b in range(b0, b1):
-                nc.vector.tensor_scalar_mul(
-                    out=belief2[:, b, :, :],
-                    in0=evidence[:, b, :].unsqueeze(1).to_broadcast([P, 2, C]),
-                    scalar1=inv_s[:, b : b + 1],
-                )
+            nc.vector.tensor_scalar_mul(
+                out=neg_half_log[:, b, :], in0=log2x[:, b, 0, :], scalar1=-0.5
+            )
 
-        def head_outputs(b0, b1):
-            blk = slice(b0, b1)
-            nc.vector.tensor_scalar_add(out=alpha[:, blk, :], in0=evidence[:, blk, :], scalar1=1.0)
-            for b in range(b0, b1):
-                nc.vector.tensor_scalar_mul(
-                    out=prob[:, b, :], in0=alpha[:, b, :], scalar1=inv_s[:, b : b + 1]
-                )
-            nc.vector.tensor_scalar_mul(out=per_row[:, blk], in0=inv_s[:, blk], scalar1=float(C))
-            nc.vector.tensor_tensor(
-                out=squares[:, blk, :], in0=belief2[:, blk, 0, :], in1=belief2[:, blk, 0, :],
-                op=ALU.mult,
-            )
-            nc.vector.tensor_reduce(
-                out=sum_sq[:, blk], in_=squares[:, blk, :], axis=AX.X, op=ALU.add
+        def head_outputs(b):
+            one = slice(b, b + 1)
+            nc.vector.tensor_scalar_add(out=alpha[:, b, :], in0=evidence[:, b, :], scalar1=1.0)
+            nc.vector.tensor_scalar_mul(out=prob[:, b, :], in0=alpha[:, b, :], scalar1=inv_s[:, one])
+            nc.vector.tensor_scalar_mul(out=per_row[:, one], in0=inv_s[:, one], scalar1=float(C))
+            nc.vector.scalar_tensor_tensor(
+                out=squares[:, b, :], in0=belief2[:, b, 0, :], scalar=1.0, in1=belief2[:, b, 0, :],
+                op0=ALU.mult, op1=ALU.mult, accum_out=sum_sq[:, one],
             )
             nc.vector.tensor_tensor(
-                out=sum_b[:, blk], in0=sum_e[:, blk], in1=inv_s[:, blk], op=ALU.mult
+                out=sum_b[:, one], in0=sum_e[:, one], in1=inv_s[:, one], op=ALU.mult
             )
-            nc.vector.tensor_tensor(
-                out=sq_of_sum[:, blk], in0=sum_b[:, blk], in1=sum_b[:, blk], op=ALU.mult
-            )
-            nc.vector.tensor_tensor(
-                out=twice_all[:, blk], in0=sq_of_sum[:, blk], in1=sum_sq[:, blk], op=ALU.subtract
+            nc.vector.scalar_tensor_tensor(
+                out=twice_all[:, one], in0=sum_b[:, one], scalar=sum_b[:, one], in1=sum_sq[:, one],
+                op0=ALU.mult, op1=ALU.subtract,
             )
 
         def run_length(c):
@@ -302,7 +283,7 @@ def tile_evidentialhead_pb_k_kernel(
             b, c = divmod(k, CHUNKS_PER_BLOCK)
             n = run_length(c)
             term = term_tiles[k]
-            if k % 2 == 0:
+            if k % 2 == 1:
                 nc.scalar.activation(
                     out=term[:, :, :n], in_=term[:, :, :n], func=ACT.Abs,
                     accum_out=part[:, 0, b, c // 2 : c // 2 + 1],
@@ -332,43 +313,39 @@ def tile_evidentialhead_pb_k_kernel(
             quantise_step(f)
         for n in range(block_banks, block_banks + BANKS_AHEAD):
             transpose_bank(n)
-        head_softplus(0, 1, acc_tiles[0])
+        head_logits(0)
+        head_log_term(0)
         evacuate_step(4)
-        head_evidence(0, 1)
+        head_evidence(0)
         quantise_step(4)
         evacuate_step(5)
-        head_pair_operands(0, 1)
-        head_outputs(0, 1)
+        head_pair_operands(0)
+        head_outputs(0)
 
-        first_step = 6
-        for k in range(CHUNKS_PER_BLOCK - 1):
+        for k in range(CHUNKS):
+            f = k + FE_LEAD
+            next_block = (k + 1) // CHUNKS_PER_BLOCK
+            with_head = (k + 1) % CHUNKS_PER_BLOCK == 0 and next_block < BLOCKS
+            if with_head:
+                head_logits(next_block)
             tanh_chunk(k)
+            if with_head:
+                head_log_term(next_block)
             weight_chunk(k)
-            lo = first_step + k * FE_STEPS_PER_CHUNK
-            for f in range(lo, min(lo + FE_STEPS_PER_CHUNK, STEPS)):
+            if f <= STEPS:
                 quantise_step(f - 1)
+            if f < STEPS:
                 evacuate_step(f)
             if k > 0:
                 abs_sum(k - 1)
-        quantise_step(STEPS - 1)
-        tanh_chunk(3)
-        weight_chunk(3)
-        abs_sum(2)
-        head_softplus(1, BLOCKS, acc_tiles[1])
-        abs_sum(3)
-        head_evidence(1, BLOCKS)
-        head_pair_operands(1, BLOCKS)
-        head_outputs(1, BLOCKS)
+            if with_head:
+                head_evidence(next_block)
+                head_pair_operands(next_block)
+                head_outputs(next_block)
+        abs_sum(CHUNKS - 1)
         nc.sync.dma_start(out=out_0.rearrange("(b p) c -> p b c", p=P), in_=alpha[:])
         nc.sync.dma_start(out=out_1.rearrange("(b p) c -> p b c", p=P), in_=evidence[:])
         nc.sync.dma_start(out=out_2.rearrange("(b p) c -> p b c", p=P), in_=prob[:])
-
-        for k in range(CHUNKS_PER_BLOCK, CHUNKS):
-            tanh_chunk(k)
-            weight_chunk(k)
-            if k > CHUNKS_PER_BLOCK:
-                abs_sum(k - 1)
-        abs_sum(CHUNKS - 1)
 
         nc.vector.tensor_reduce(
             out=total[:], in_=part[:].rearrange("p e b j -> p b e j"), axis=AX.XY, op=ALU.add

@@ -19,6 +19,7 @@ ROWS = 512
 K_DIM = 16384
 C = 128
 EPS_B = 1e-8
+TINY = 1e-18
 FLOPS = 2 * ROWS * K_DIM * C
 
 BLOCKS = ROWS // P
@@ -35,13 +36,13 @@ STEP_BANKS = STEP_GROUPS // BANK_GROUPS
 BANKS = STEPS * STEP_BANKS
 BANKS_AHEAD = 6
 H_BUFS = 8
+W_PIECES = 4
 
 HALF = C // 2
 CHUNK_I = 32
 CHUNKS_PER_BLOCK = C // CHUNK_I
 CHUNKS = BLOCKS * CHUNKS_PER_BLOCK
-FE_LEAD = 6
-W_PIECES = 4
+FE_LEAD = 7
 
 
 def tile_evidentialhead_pb_k_kernel(
@@ -61,30 +62,30 @@ def tile_evidentialhead_pb_k_kernel(
         stack.enter_context(tc.manual_schedule())
 
         ident = const.tile([P, P], F32, name="ident")
+        warm = const.tile([P, 2], F32, name="warm")
         w_words = const.tile([P, GROUPS, 2 * C], U8, name="w_words", align_bytes=64)
         w_planes = const.tile([P, GROUPS, C], U8, name="w_planes", align_bytes=64)
         b3_all = const.tile([P, C], BF16, name="b3_all")
 
         logits = const.tile([P, BLOCKS, C], F32, name="logits")
-        neg_abs = const.tile([P, BLOCKS, C], F32, name="neg_abs")
-        decay = const.tile([P, BLOCKS, C], F32, name="decay")
-        log_term = const.tile([P, BLOCKS, C], F32, name="log_term")
+        abs_z = const.tile([P, BLOCKS, C], F32, name="abs_z")
+        sig_z = const.tile([P, BLOCKS, C], F32, name="sig_z")
+        ln_sig = const.tile([P, BLOCKS, C], F32, name="ln_sig")
         evidence = const.tile([P, BLOCKS, C], F32, name="evidence")
         alpha = const.tile([P, BLOCKS, C], F32, name="alpha")
         prob = const.tile([P, BLOCKS, C], F32, name="prob")
-        squares = const.tile([P, BLOCKS, C], F32, name="squares")
-        log2x = const.tile([P, BLOCKS, 2, C], F32, name="log2x")
-        belief2 = const.tile([P, BLOCKS, 2, C], F32, name="belief2")
-        neg_half_log = const.tile([P, BLOCKS, C], F32, name="neg_half_log")
+        ln_e2 = const.tile([P, BLOCKS, 2, C], F32, name="ln_e2")
+        ln_ec = const.tile([P, BLOCKS, C], F32, name="ln_ec")
+        neg_ln_ec = const.tile([P, BLOCKS, C], F32, name="neg_ln_ec")
+        belief = const.tile([P, BLOCKS, C], F32, name="belief")
+        belief_h2 = const.tile([P, BLOCKS, 2, C], F32, name="belief_h2")
+        cap = const.tile([P, BLOCKS, C], F32, name="cap")
         sum_e = const.tile([P, BLOCKS], F32, name="sum_e")
-        half_eps = const.tile([P, BLOCKS], F32, name="half_eps")
+        c_eps = const.tile([P, BLOCKS], F32, name="c_eps")
+        half_c = const.tile([P, BLOCKS], F32, name="half_c")
         strength = const.tile([P, BLOCKS], F32, name="strength")
         inv_s = const.tile([P, BLOCKS], F32, name="inv_s")
-        sum_b = const.tile([P, BLOCKS], F32, name="sum_b")
-        sum_sq = const.tile([P, BLOCKS], F32, name="sum_sq")
-        twice_all = const.tile([P, BLOCKS], F32, name="twice_all")
-        part = const.tile([P, 2, BLOCKS, CHUNKS_PER_BLOCK // 2], F32, name="part")
-        total = const.tile([P, BLOCKS], F32, name="total")
+        part = const.tile([P, BLOCKS, CHUNKS_PER_BLOCK], F32, name="part")
         per_row = const.tile([P, P], F32, name="per_row")
         per_row_t = const.tile([P, P], F32, name="per_row_t")
 
@@ -93,8 +94,8 @@ def tile_evidentialhead_pb_k_kernel(
         grouped_tiles = {}
         code_tiles = {}
         acc_tiles = {}
-        tanh_tiles = {}
-        term_tiles = {}
+        ratio_tiles = {}
+        weight_tiles = {}
 
         def load_chunk(f):
             b, q = divmod(f, STEPS_PER_BLOCK)
@@ -132,7 +133,7 @@ def tile_evidentialhead_pb_k_kernel(
                     )
             banks[n] = xt
 
-        def evacuate_step(f, refill_end=BANKS):
+        def evacuate_step(f, vector_banks, refill_end=BANKS):
             grouped = grouped_pool.tile([P, STEP_K], BF16, name="grouped", align_bytes=64)
             grouped_tiles[f] = grouped
             dst = grouped[:].bitcast(F32).rearrange(
@@ -141,7 +142,7 @@ def tile_evidentialhead_pb_k_kernel(
             for j in range(STEP_BANKS):
                 n = f * STEP_BANKS + j
                 src = banks[n][:].rearrange("p g u r -> p g r u")
-                if j == STEP_BANKS - 1:
+                if j >= STEP_BANKS - vector_banks:
                     nc.vector.tensor_copy(out=dst[:, j], in_=src)
                 else:
                     nc.scalar.copy(out=dst[:, j], in_=src)
@@ -187,117 +188,107 @@ def tile_evidentialhead_pb_k_kernel(
                 out=logits[:, b, :], in0=acc_tiles[b][:], in1=b3_all[:], op=ALU.add
             )
             nc.vector.scalar_tensor_tensor(
-                out=neg_abs[:, b, :], in0=logits[:, b, :], scalar=-1.0, in1=logits[:, b, :],
-                op0=ALU.mult, op1=ALU.min,
+                out=abs_z[:, b, :], in0=logits[:, b, :], scalar=-1.0, in1=logits[:, b, :],
+                op0=ALU.mult, op1=ALU.max,
             )
 
         def head_log_term(b):
-            nc.scalar.activation(out=decay[:, b, :], in_=neg_abs[:, b, :], func=ACT.Exp)
-            nc.scalar.activation(out=log_term[:, b, :], in_=decay[:, b, :], func=ACT.Ln, bias=1.0)
+            nc.scalar.activation(out=sig_z[:, b, :], in_=abs_z[:, b, :], func=ACT.Sigmoid)
+            nc.scalar.activation(out=ln_sig[:, b, :], in_=sig_z[:, b, :], func=ACT.Ln)
 
         def head_evidence(b):
             one = slice(b, b + 1)
             nc.vector.scalar_tensor_tensor(
-                out=evidence[:, b, :], in0=logits[:, b, :], scalar=0.0, in1=log_term[:, b, :],
-                op0=ALU.max, op1=ALU.add, accum_out=sum_e[:, one],
+                out=evidence[:, b, :], in0=logits[:, b, :], scalar=0.0, in1=ln_sig[:, b, :],
+                op0=ALU.max, op1=ALU.subtract, accum_out=sum_e[:, one],
             )
             nc.vector.tensor_scalar(
-                out=half_eps[:, one], in0=sum_e[:, one], scalar1=float(C),
-                scalar2=0.5 * EPS_B, op0=ALU.add, op1=ALU.mult,
+                out=c_eps[:, one], in0=sum_e[:, one], scalar1=float(C), scalar2=EPS_B,
+                op0=ALU.add, op1=ALU.mult,
             )
             nc.scalar.activation(
-                out=log2x[:, b, :, :],
+                out=ln_e2[:, b, :, :],
                 in_=evidence[:, b, :].unsqueeze(1).to_broadcast([P, 2, C]),
                 func=ACT.Ln,
-                bias=half_eps[:, one],
+                bias=TINY,
+            )
+            nc.scalar.activation(
+                out=ln_ec[:, b, :], in_=evidence[:, b, :], func=ACT.Ln, bias=c_eps[:, one]
             )
 
         def head_pair_operands(b):
             one = slice(b, b + 1)
             nc.vector.tensor_scalar_add(out=strength[:, one], in0=sum_e[:, one], scalar1=float(C))
             nc.vector.reciprocal(out=inv_s[:, one], in_=strength[:, one])
+            nc.vector.tensor_scalar_mul(out=half_c[:, one], in0=c_eps[:, one], scalar1=0.5)
             nc.vector.tensor_scalar_mul(
-                out=belief2[:, b, :, :],
+                out=belief[:, b, :], in0=evidence[:, b, :], scalar1=inv_s[:, one]
+            )
+            nc.vector.tensor_scalar(
+                out=belief_h2[:, b, :, :],
                 in0=evidence[:, b, :].unsqueeze(1).to_broadcast([P, 2, C]),
-                scalar1=inv_s[:, one],
+                scalar1=half_c[:, one], scalar2=inv_s[:, one], op0=ALU.add, op1=ALU.mult,
             )
-            nc.vector.tensor_scalar_mul(
-                out=neg_half_log[:, b, :], in0=log2x[:, b, 0, :], scalar1=-0.5
+            nc.vector.tensor_tensor(
+                out=cap[:, b, :], in0=belief[:, b, :], in1=belief_h2[:, b, 0, :], op=ALU.mult
             )
+            nc.vector.tensor_scalar_mul(out=neg_ln_ec[:, b, :], in0=ln_ec[:, b, :], scalar1=-1.0)
 
         def head_outputs(b):
             one = slice(b, b + 1)
             nc.vector.tensor_scalar_add(out=alpha[:, b, :], in0=evidence[:, b, :], scalar1=1.0)
             nc.vector.tensor_scalar_mul(out=prob[:, b, :], in0=alpha[:, b, :], scalar1=inv_s[:, one])
             nc.vector.tensor_scalar_mul(out=per_row[:, one], in0=inv_s[:, one], scalar1=float(C))
-            nc.vector.scalar_tensor_tensor(
-                out=squares[:, b, :], in0=belief2[:, b, 0, :], scalar=1.0, in1=belief2[:, b, 0, :],
-                op0=ALU.mult, op1=ALU.mult, accum_out=sum_sq[:, one],
-            )
-            nc.vector.tensor_tensor(
-                out=sum_b[:, one], in0=sum_e[:, one], in1=inv_s[:, one], op=ALU.mult
-            )
-            nc.vector.scalar_tensor_tensor(
-                out=twice_all[:, one], in0=sum_b[:, one], scalar=sum_b[:, one], in1=sum_sq[:, one],
-                op0=ALU.mult, op1=ALU.subtract,
-            )
 
         def run_length(c):
             return HALF if c * CHUNK_I < HALF else HALF - 1
 
-        def tanh_chunk(k):
+        def ratio_chunk(k):
             b, c = divmod(k, CHUNKS_PER_BLOCK)
             n = run_length(c)
-            logs = log2x[:, b, :, :].rearrange("p d c -> p (d c)")
-            tanh_t = pair_pool.tile([P, CHUNK_I, HALF], F32, name="tanh_t")
-            tanh_tiles[k] = tanh_t
+            logs = ln_e2[:, b, :, :].rearrange("p d c -> p (d c)")
+            ratio = pair_pool.tile([P, CHUNK_I * HALF], F32, name="ratio")
+            ratio_tiles[k] = ratio
             for ii in range(CHUNK_I):
                 i = c * CHUNK_I + ii
                 nc.scalar.activation(
-                    out=tanh_t[:, ii, :n],
+                    out=ratio[:, ii * n : (ii + 1) * n],
                     in_=logs[:, i + 1 : i + 1 + n],
-                    func=ACT.Tanh,
-                    scale=0.5,
-                    bias=neg_half_log[:, b, i : i + 1],
+                    func=ACT.Sigmoid,
+                    bias=neg_ln_ec[:, b, i : i + 1],
                 )
 
         def weight_chunk(k):
             b, c = divmod(k, CHUNKS_PER_BLOCK)
             n = run_length(c)
-            beliefs = belief2[:, b, :, :].rearrange("p d c -> p (d c)")
-            tanh_t = tanh_tiles[k]
-            term = pair_pool.tile([P, CHUNK_I, HALF], F32, name="term")
-            term_tiles[k] = term
+            partners = belief_h2[:, b, :, :].rearrange("p d c -> p (d c)")
+            weight = pair_pool.tile([P, CHUNK_I * HALF], F32, name="weight")
+            weight_tiles[k] = weight
             for ii in range(CHUNK_I):
                 i = c * CHUNK_I + ii
-                nc.vector.scalar_tensor_tensor(
-                    out=term[:, ii, :n],
-                    in0=tanh_t[:, ii, :n],
-                    scalar=beliefs[:, i : i + 1],
-                    in1=beliefs[:, i + 1 : i + 1 + n],
+                nc.vector.tensor_scalar(
+                    out=weight[:, ii * n : (ii + 1) * n],
+                    in0=partners[:, i + 1 : i + 1 + n],
+                    scalar1=belief[:, b, i : i + 1],
+                    scalar2=cap[:, b, i : i + 1],
                     op0=ALU.mult,
-                    op1=ALU.mult,
+                    op1=ALU.min,
                 )
 
-        def abs_sum(k):
+        def sum_chunk(k):
             b, c = divmod(k, CHUNKS_PER_BLOCK)
-            n = run_length(c)
-            term = term_tiles[k]
-            if k % 2 == 1:
-                nc.scalar.activation(
-                    out=term[:, :, :n], in_=term[:, :, :n], func=ACT.Abs,
-                    accum_out=part[:, 0, b, c // 2 : c // 2 + 1],
-                )
-            else:
-                nc.vector.scalar_tensor_tensor(
-                    out=term[:, :, :n], in0=term[:, :, :n], scalar=-1.0, in1=term[:, :, :n],
-                    op0=ALU.mult, op1=ALU.max,
-                    accum_out=part[:, 1, b, c // 2 : c // 2 + 1],
-                )
+            used = slice(0, CHUNK_I * run_length(c))
+            weight = weight_tiles[k]
+            nc.vector.scalar_tensor_tensor(
+                out=weight[:, used], in0=weight[:, used], scalar=2.0, in1=ratio_tiles[k][:, used],
+                op0=ALU.mult, op1=ALU.mult, accum_out=part[:, b, c : c + 1],
+            )
 
         nc.vector.memset(w_planes[:].bitcast(I32), 0)
         make_identity(nc, ident[:])
         nc.gpsimd.memset(per_row[:], 0.0)
+        nc.gpsimd.memset(warm[:], 0.0)
+        nc.scalar.activation(out=warm[:, 1:2], in_=warm[:, 0:1], func=ACT.Sigmoid)
         nc.scalar.dma_start(out=b3_all[:], in_=b3.partition_broadcast(P))
         for f in range(STEPS_PER_BLOCK):
             load_chunk(f)
@@ -309,18 +300,20 @@ def tile_evidentialhead_pb_k_kernel(
 
         block_banks = STEPS_PER_BLOCK * STEP_BANKS
         for f in range(STEPS_PER_BLOCK):
-            evacuate_step(f, refill_end=block_banks)
+            evacuate_step(f, vector_banks=2, refill_end=block_banks)
             quantise_step(f)
         for n in range(block_banks, block_banks + BANKS_AHEAD):
             transpose_bank(n)
         head_logits(0)
         head_log_term(0)
-        evacuate_step(4)
+        evacuate_step(4, vector_banks=2)
         head_evidence(0)
         quantise_step(4)
-        evacuate_step(5)
+        evacuate_step(5, vector_banks=2)
         head_pair_operands(0)
         head_outputs(0)
+        quantise_step(5)
+        evacuate_step(6, vector_banks=2)
 
         for k in range(CHUNKS):
             f = k + FE_LEAD
@@ -328,31 +321,27 @@ def tile_evidentialhead_pb_k_kernel(
             with_head = (k + 1) % CHUNKS_PER_BLOCK == 0 and next_block < BLOCKS
             if with_head:
                 head_logits(next_block)
-            tanh_chunk(k)
+            ratio_chunk(k)
             if with_head:
                 head_log_term(next_block)
             weight_chunk(k)
             if f <= STEPS:
                 quantise_step(f - 1)
             if f < STEPS:
-                evacuate_step(f)
+                evacuate_step(f, vector_banks=0)
             if k > 0:
-                abs_sum(k - 1)
+                sum_chunk(k - 1)
             if with_head:
                 head_evidence(next_block)
                 head_pair_operands(next_block)
                 head_outputs(next_block)
-        abs_sum(CHUNKS - 1)
+        sum_chunk(CHUNKS - 1)
         nc.sync.dma_start(out=out_0.rearrange("(b p) c -> p b c", p=P), in_=alpha[:])
         nc.sync.dma_start(out=out_1.rearrange("(b p) c -> p b c", p=P), in_=evidence[:])
         nc.sync.dma_start(out=out_2.rearrange("(b p) c -> p b c", p=P), in_=prob[:])
 
         nc.vector.tensor_reduce(
-            out=total[:], in_=part[:].rearrange("p e b j -> p b e j"), axis=AX.XY, op=ALU.add
-        )
-        nc.vector.scalar_tensor_tensor(
-            out=per_row[:, BLOCKS : 2 * BLOCKS], in0=twice_all[:], scalar=0.5, in1=total[:],
-            op0=ALU.mult, op1=ALU.subtract,
+            out=per_row[:, BLOCKS : 2 * BLOCKS], in_=part[:], axis=AX.X, op=ALU.add
         )
         turned = psum_t.tile([P, P], F32, name="turned", tag="xt")
         nc.tensor.transpose(turned[:], per_row[:], ident[:])

@@ -103,14 +103,16 @@ def tile_evidentialhead_pb_k_kernel(
             nc.sync.dma_start(out=h_chunk[:], in_=h_rows[:, b, q * STEP_K : (q + 1) * STEP_K])
             chunks[f] = h_chunk
 
-        def load_weights():
-            scale_words = W3_scales.bitcast(I32)
+        def load_scales():
+            scale_words = W3_scales.bitcast(F32)
             for first in range(8):
                 part0 = 32 * (first // 4) + first % 4
-                nc.sync.dma_start(
-                    out=w_planes[part0:P:64, :, :].bitcast(I32),
+                nc.gpsimd.dma_start(
+                    out=w_planes[part0:P:64, :, :].bitcast(F32),
                     in_=scale_words[:, first:16:8, :].rearrange("g q n -> q g n"),
                 )
+
+        def load_words():
             words = W3_words.bitcast(I32).rearrange("g p n -> p g n")
             piece = GROUPS // W_PIECES
             for g0 in range(0, GROUPS, piece):
@@ -290,9 +292,10 @@ def tile_evidentialhead_pb_k_kernel(
         nc.gpsimd.memset(warm[:], 0.0)
         nc.scalar.activation(out=warm[:, 1:2], in_=warm[:, 0:1], func=ACT.Sigmoid)
         nc.scalar.dma_start(out=b3_all[:], in_=b3.partition_broadcast(P))
+        load_scales()
         for f in range(STEPS_PER_BLOCK):
             load_chunk(f)
-        load_weights()
+        load_words()
         for f in range(STEPS_PER_BLOCK, H_BUFS):
             load_chunk(f)
         for n in range(BANKS_AHEAD):

@@ -43,6 +43,7 @@ CHUNK_I = 32
 CHUNKS_PER_BLOCK = C // CHUNK_I
 CHUNKS = BLOCKS * CHUNKS_PER_BLOCK
 FE_LEAD = 7
+FIRST_STEPS = 6
 
 
 def tile_evidentialhead_pb_k_kernel(
@@ -54,7 +55,7 @@ def tile_evidentialhead_pb_k_kernel(
     with ExitStack() as stack:
         const = stack.enter_context(tc.tile_pool(name="const", bufs=1))
         h_pool = stack.enter_context(tc.tile_pool(name="h", bufs=H_BUFS))
-        grouped_pool = stack.enter_context(tc.tile_pool(name="grouped", bufs=2))
+        grouped_pool = stack.enter_context(tc.tile_pool(name="grouped", bufs=3))
         codes_pool = stack.enter_context(tc.tile_pool(name="codes", bufs=2))
         pair_pool = stack.enter_context(tc.tile_pool(name="pair", bufs=3))
         psum_t = stack.enter_context(tc.psum_pool(name="psum_t", bufs=BANKS_AHEAD))
@@ -103,16 +104,13 @@ def tile_evidentialhead_pb_k_kernel(
             nc.sync.dma_start(out=h_chunk[:], in_=h_rows[:, b, q * STEP_K : (q + 1) * STEP_K])
             chunks[f] = h_chunk
 
-        def load_scales():
-            scale_words = W3_scales.bitcast(F32)
-            for first in range(8):
-                part0 = 32 * (first // 4) + first % 4
-                nc.gpsimd.dma_start(
-                    out=w_planes[part0:P:64, :, :].bitcast(F32),
-                    in_=scale_words[:, first:16:8, :].rearrange("g q n -> q g n"),
+        def load_weights():
+            scale_words = W3_scales.bitcast(I32)
+            for quad in range(4):
+                nc.sync.dma_start(
+                    out=w_planes[32 * quad : 32 * quad + 4, :, :].bitcast(I32),
+                    in_=scale_words[:, 4 * quad : 4 * quad + 4, :].rearrange("g q n -> q g n"),
                 )
-
-        def load_words():
             words = W3_words.bitcast(I32).rearrange("g p n -> p g n")
             piece = GROUPS // W_PIECES
             for g0 in range(0, GROUPS, piece):
@@ -120,6 +118,7 @@ def tile_evidentialhead_pb_k_kernel(
                     out=w_words[:, g0 : g0 + piece, :].bitcast(I32),
                     in_=words[:, g0 : g0 + piece, :],
                 )
+            nc.sync.dma_start(out=b3_all[:], in_=b3.partition_broadcast(P))
 
         def transpose_bank(n):
             f, j = divmod(n, STEP_BANKS)
@@ -291,11 +290,9 @@ def tile_evidentialhead_pb_k_kernel(
         nc.gpsimd.memset(per_row[:], 0.0)
         nc.gpsimd.memset(warm[:], 0.0)
         nc.scalar.activation(out=warm[:, 1:2], in_=warm[:, 0:1], func=ACT.Sigmoid)
-        nc.scalar.dma_start(out=b3_all[:], in_=b3.partition_broadcast(P))
-        load_scales()
         for f in range(STEPS_PER_BLOCK):
             load_chunk(f)
-        load_words()
+        load_weights()
         for f in range(STEPS_PER_BLOCK, H_BUFS):
             load_chunk(f)
         for n in range(BANKS_AHEAD):
@@ -309,17 +306,16 @@ def tile_evidentialhead_pb_k_kernel(
             transpose_bank(n)
         head_logits(0)
         head_log_term(0)
-        evacuate_step(4, vector_banks=2)
         head_evidence(0)
-        quantise_step(4)
-        evacuate_step(5, vector_banks=2)
         head_pair_operands(0)
         head_outputs(0)
-        quantise_step(5)
-        evacuate_step(6, vector_banks=2)
+        evacuate_step(STEPS_PER_BLOCK, vector_banks=STEP_BANKS)
+        for f in range(STEPS_PER_BLOCK + 1, FIRST_STEPS):
+            quantise_step(f - 1)
+            evacuate_step(f, vector_banks=STEP_BANKS)
 
+        copied = FIRST_STEPS
         for k in range(CHUNKS):
-            f = k + FE_LEAD
             next_block = (k + 1) // CHUNKS_PER_BLOCK
             with_head = (k + 1) % CHUNKS_PER_BLOCK == 0 and next_block < BLOCKS
             if with_head:
@@ -328,10 +324,11 @@ def tile_evidentialhead_pb_k_kernel(
             if with_head:
                 head_log_term(next_block)
             weight_chunk(k)
-            if f <= STEPS:
+            for f in range(copied, min(k + FE_LEAD, STEPS) + 1):
                 quantise_step(f - 1)
-            if f < STEPS:
-                evacuate_step(f, vector_banks=0)
+                if f < STEPS:
+                    evacuate_step(f, vector_banks=0)
+            copied = max(copied, min(k + FE_LEAD, STEPS) + 1)
             if k > 0:
                 sum_chunk(k - 1)
             if with_head:

@@ -1,4 +1,5 @@
 from contextlib import ExitStack
+from functools import partial
 
 import concourse.mybir as mybir
 from concourse.masks import make_identity
@@ -35,15 +36,15 @@ BANK_GROUPS = 2
 STEP_BANKS = STEP_GROUPS // BANK_GROUPS
 BANKS = STEPS * STEP_BANKS
 BANKS_AHEAD = 6
-H_BUFS = 8
+H_BUFS = 7
 W_PIECES = 4
 
 HALF = C // 2
 CHUNK_I = 32
-CHUNKS_PER_BLOCK = C // CHUNK_I
-CHUNKS = BLOCKS * CHUNKS_PER_BLOCK
-FE_LEAD = 7
-FIRST_STEPS = 6
+CHUNKS = C // CHUNK_I
+RATIOS_PER_COPY = 5
+RANKS = 4
+LANE = C // RANKS
 
 
 def tile_evidentialhead_pb_k_kernel(
@@ -57,7 +58,10 @@ def tile_evidentialhead_pb_k_kernel(
         h_pool = stack.enter_context(tc.tile_pool(name="h", bufs=H_BUFS))
         grouped_pool = stack.enter_context(tc.tile_pool(name="grouped", bufs=3))
         codes_pool = stack.enter_context(tc.tile_pool(name="codes", bufs=2))
-        pair_pool = stack.enter_context(tc.tile_pool(name="pair", bufs=3))
+        ratio_pool = stack.enter_context(tc.tile_pool(name="ratio", bufs=CHUNKS))
+        weight_pool = stack.enter_context(tc.tile_pool(name="weight", bufs=2))
+        head_pool = stack.enter_context(tc.tile_pool(name="head", bufs=2))
+        sort_pool = stack.enter_context(tc.tile_pool(name="sort", bufs=4))
         psum_t = stack.enter_context(tc.psum_pool(name="psum_t", bufs=BANKS_AHEAD))
         psum_acc = stack.enter_context(tc.psum_pool(name="psum_acc", bufs=2))
         stack.enter_context(tc.manual_schedule())
@@ -67,26 +71,26 @@ def tile_evidentialhead_pb_k_kernel(
         w_words = const.tile([P, GROUPS, 2 * C], U8, name="w_words", align_bytes=64)
         w_planes = const.tile([P, GROUPS, C], U8, name="w_planes", align_bytes=64)
         b3_all = const.tile([P, C], BF16, name="b3_all")
+        unused = const.tile([P, 16 * C], F32, name="unused")
 
-        logits = const.tile([P, BLOCKS, C], F32, name="logits")
-        abs_z = const.tile([P, BLOCKS, C], F32, name="abs_z")
-        sig_z = const.tile([P, BLOCKS, C], F32, name="sig_z")
-        ln_sig = const.tile([P, BLOCKS, C], F32, name="ln_sig")
-        evidence = const.tile([P, BLOCKS, C], F32, name="evidence")
+        logits = const.tile([P, BLOCKS, 2, C], F32, name="logits")
+        evidence = const.tile([P, BLOCKS, 2, C], F32, name="evidence")
         alpha = const.tile([P, BLOCKS, C], F32, name="alpha")
         prob = const.tile([P, BLOCKS, C], F32, name="prob")
-        ln_e2 = const.tile([P, BLOCKS, 2, C], F32, name="ln_e2")
+        ln_e0 = const.tile([P, 2, C], F32, name="ln_e0")
+        ln_e = const.tile([P, BLOCKS, C], F32, name="ln_e")
         ln_ec = const.tile([P, BLOCKS, C], F32, name="ln_ec")
         neg_ln_ec = const.tile([P, BLOCKS, C], F32, name="neg_ln_ec")
         belief = const.tile([P, BLOCKS, C], F32, name="belief")
         belief_h2 = const.tile([P, BLOCKS, 2, C], F32, name="belief_h2")
         cap = const.tile([P, BLOCKS, C], F32, name="cap")
+        above = const.tile([P, BLOCKS, C], F32, name="above")
         sum_e = const.tile([P, BLOCKS], F32, name="sum_e")
         c_eps = const.tile([P, BLOCKS], F32, name="c_eps")
         half_c = const.tile([P, BLOCKS], F32, name="half_c")
         strength = const.tile([P, BLOCKS], F32, name="strength")
         inv_s = const.tile([P, BLOCKS], F32, name="inv_s")
-        part = const.tile([P, BLOCKS, CHUNKS_PER_BLOCK], F32, name="part")
+        part = const.tile([P, CHUNKS], F32, name="part")
         per_row = const.tile([P, P], F32, name="per_row")
         per_row_t = const.tile([P, P], F32, name="per_row_t")
 
@@ -95,6 +99,8 @@ def tile_evidentialhead_pb_k_kernel(
         grouped_tiles = {}
         code_tiles = {}
         acc_tiles = {}
+        abs_tiles = {}
+        ln_sig_tiles = {}
         ratio_tiles = {}
         weight_tiles = {}
 
@@ -134,48 +140,63 @@ def tile_evidentialhead_pb_k_kernel(
                     )
             banks[n] = xt
 
-        def evacuate_step(f, vector_banks, refill_end=BANKS):
-            grouped = grouped_pool.tile([P, STEP_K], BF16, name="grouped", align_bytes=64)
-            grouped_tiles[f] = grouped
-            dst = grouped[:].bitcast(F32).rearrange(
+        def grouped_view(f):
+            if f not in grouped_tiles:
+                grouped = grouped_pool.tile([P, STEP_K], BF16, name="grouped", align_bytes=64)
+                grouped_tiles[f] = grouped
+            return grouped_tiles[f][:].bitcast(F32).rearrange(
                 "p (j g r u) -> p j g r u", j=STEP_BANKS, g=BANK_GROUPS, u=2
             )
-            for j in range(STEP_BANKS):
-                n = f * STEP_BANKS + j
-                src = banks[n][:].rearrange("p g u r -> p g r u")
-                if j >= STEP_BANKS - vector_banks:
-                    nc.vector.tensor_copy(out=dst[:, j], in_=src)
-                else:
-                    nc.scalar.copy(out=dst[:, j], in_=src)
-                if n + BANKS_AHEAD < refill_end:
-                    transpose_bank(n + BANKS_AHEAD)
-            if f + H_BUFS < STEPS:
+
+        def bank_done(n, refill_end):
+            if n + BANKS_AHEAD < refill_end:
+                transpose_bank(n + BANKS_AHEAD)
+            f, j = divmod(n, STEP_BANKS)
+            if j == STEP_BANKS - 1 and f + H_BUFS < STEPS:
                 load_chunk(f + H_BUFS)
 
-        def quantise_step(f):
+        def copy_bank(n, engine, refill_end=BANKS):
+            f, j = divmod(n, STEP_BANKS)
+            dst = grouped_view(f)[:, j]
+            src = banks[n][:].rearrange("p g u r -> p g r u")
+            if engine == "scalar":
+                nc.scalar.copy(out=dst, in_=src)
+            else:
+                nc.vector.tensor_copy(out=dst, in_=src)
+            bank_done(n, refill_end)
+
+        def copy_half_bank(n, g):
+            f, j = divmod(n, STEP_BANKS)
+            nc.vector.tensor_copy(
+                out=grouped_view(f)[:, j, g], in_=banks[n][:, g].rearrange("p u r -> p r u")
+            )
+            if g == BANK_GROUPS - 1:
+                bank_done(n, BANKS)
+
+        def quantise(f, g0, g1):
             b, q = divmod(f, STEPS_PER_BLOCK)
-            if q == 0:
+            if q == 0 and g0 == 0:
                 h_codes = codes_pool.tile([P, GROUPS * P], U32, name="h_codes", align_bytes=64)
                 h_scales = codes_pool.tile([P, GROUPS * P], U8, name="h_scales", align_bytes=64)
                 code_tiles[b] = (h_codes, h_scales)
             h_codes, h_scales = code_tiles[b]
-            cols = slice(q * STEP_GROUPS * P, (q + 1) * STEP_GROUPS * P)
+            cols = slice((q * STEP_GROUPS + g0) * P, (q * STEP_GROUPS + g1) * P)
             nc.vector.quantize_mx(
                 out=h_codes[:, cols].bitcast(FP8X4),
                 scales=h_scales[:, cols],
-                in_=grouped_tiles[f][:],
+                in_=grouped_tiles[f][:, g0 * K_PASS : g1 * K_PASS],
             )
-            if q == STEPS_PER_BLOCK - 1:
-                mx_block(b)
 
-        def mx_block(b):
-            acc = psum_acc.tile([P, C], F32, name="acc")
-            acc_tiles[b] = acc
+        def multiply(f, g0, g1):
+            b, q = divmod(f, STEPS_PER_BLOCK)
+            if q == 0 and g0 == 0:
+                acc = psum_acc.tile([P, C], F32, name="acc")
+                acc_tiles[b] = acc
             h_codes, h_scales = code_tiles[b]
-            for g in range(GROUPS):
+            for g in range(q * STEP_GROUPS + g0, q * STEP_GROUPS + g1):
                 rows = slice(g * P, (g + 1) * P)
                 nc.tensor.matmul_mx(
-                    out=acc[:],
+                    out=acc_tiles[b][:],
                     lhsT=h_codes[:, rows].bitcast(FP8X4),
                     lhsT_scale=h_scales[:, rows],
                     rhs=w_words[:, g, :].bitcast(FP4X4),
@@ -184,110 +205,245 @@ def tile_evidentialhead_pb_k_kernel(
                     stop=(g == GROUPS - 1),
                 )
 
+        def vector_front_end(b):
+            half = STEP_GROUPS // 2
+            pieces = []
+
+            def quantise_half(f, g0):
+                quantise(f, g0, g0 + half)
+                multiply(f, g0, g0 + half)
+
+            for f in range(b * STEPS_PER_BLOCK, (b + 1) * STEPS_PER_BLOCK):
+                for j in range(STEP_BANKS):
+                    for g in range(BANK_GROUPS):
+                        pieces.append(partial(copy_half_bank, f * STEP_BANKS + j, g))
+                        if f > b * STEPS_PER_BLOCK and j < 2 and g == 1:
+                            pieces.append(partial(quantise_half, f - 1, j * half))
+            for g0 in (0, half):
+                pieces.append(partial(quantise_half, (b + 1) * STEPS_PER_BLOCK - 1, g0))
+            return pieces
+
+        def sort_steps(b):
+            steps = []
+            state = {"src": logits[:, b, 0, :]}
+
+            def compare(hi0, hi1, pick, last=False):
+                def step():
+                    src = state["src"]
+                    if last:
+                        dst = logits[:, b, 1, :]
+                    else:
+                        buf = sort_pool.tile([P, C], F32, name="buf")
+                        dst = buf[:]
+                    for half, op in ((0, ALU.max), (1, ALU.min)):
+                        nc.vector.tensor_tensor(
+                            out=pick(dst, half), in0=hi0(src), in1=hi1(src), op=op
+                        )
+                    state["src"] = dst
+
+                steps.append(step)
+
+            compare(
+                lambda s: s[:, 0:HALF],
+                lambda s: s[:, HALF:C],
+                lambda d, half: d[:, half * HALF : (half + 1) * HALF],
+            )
+            compare(
+                lambda s: s.rearrange("p (z o r) -> p z o r", z=2, o=2)[:, :, 0, :],
+                lambda s: s.rearrange("p (z o r) -> p z o r", z=2, o=2)[:, ::-1, 1, :],
+                lambda d, half: d[:, half * HALF : (half + 1) * HALF].rearrange(
+                    "p (z r) -> p z r", z=2
+                ),
+            )
+            compare(
+                lambda s: s.rearrange("p (o z r) -> p o z r", o=2, z=2)[:, :, 0, :],
+                lambda s: s.rearrange("p (o z r) -> p o z r", o=2, z=2)[:, :, 1, :],
+                lambda d, half: d.rearrange("p (o z r) -> p o z r", o=2, z=2)[:, :, half, :],
+            )
+            for top in range(2, 7):
+                m = 2 ** (top - 2)
+                lanes = dict(q=RANKS, t=2, m=m)
+                compare(
+                    lambda s, lanes=lanes: s.rearrange(
+                        "p (q h t m) -> p h t m q", **lanes
+                    )[:, :, 0, :, :],
+                    lambda s, lanes=lanes: s.rearrange(
+                        "p (q h t m) -> p h t m q", **lanes
+                    )[:, :, 1, ::-1, ::-1],
+                    lambda d, half, lanes=lanes: d.rearrange(
+                        "p (h t m q) -> p h t m q", **lanes
+                    )[:, :, half, :, :],
+                )
+                for bit in range(top - 1, 1, -1):
+                    view = dict(t=2, s=2**bit)
+                    compare(
+                        lambda s, view=view: s.rearrange("p (h t s) -> p h t s", **view)[:, :, 0, :],
+                        lambda s, view=view: s.rearrange("p (h t s) -> p h t s", **view)[:, :, 1, :],
+                        lambda d, half, view=view: d.rearrange(
+                            "p (h t s) -> p h t s", **view
+                        )[:, :, half, :],
+                    )
+                compare(
+                    lambda s: s.rearrange("p (r o z) -> p r o z", o=2, z=2)[:, :, 0, :],
+                    lambda s: s.rearrange("p (r o z) -> p r o z", o=2, z=2)[:, :, 1, :],
+                    lambda d, half: d[:, half * HALF : (half + 1) * HALF].rearrange(
+                        "p (r z) -> p r z", z=2
+                    ),
+                )
+                if top < 6:
+                    compare(
+                        lambda s: s.rearrange("p (o r z) -> p o z r", o=2, z=2)[:, :, 0, :],
+                        lambda s: s.rearrange("p (o r z) -> p o z r", o=2, z=2)[:, :, 1, :],
+                        lambda d, half: d.rearrange("p (o z r) -> p o z r", o=2, z=2)[:, :, half, :],
+                    )
+                else:
+                    compare(
+                        lambda s: s.rearrange("p (o r z) -> p z r o", o=2, z=2)[:, 0, :, :],
+                        lambda s: s.rearrange("p (o r z) -> p z r o", o=2, z=2)[:, 1, :, :],
+                        lambda d, half: d.rearrange("p (r o z) -> p z r o", o=2, z=2)[:, half, :, :],
+                        last=True,
+                    )
+            return steps
+
+        def halves(b):
+            return 1 if b == 0 else 2
+
         def head_logits(b):
             nc.vector.tensor_tensor(
-                out=logits[:, b, :], in0=acc_tiles[b][:], in1=b3_all[:], op=ALU.add
-            )
-            nc.vector.scalar_tensor_tensor(
-                out=abs_z[:, b, :], in0=logits[:, b, :], scalar=-1.0, in1=logits[:, b, :],
-                op0=ALU.mult, op1=ALU.max,
+                out=logits[:, b, 0, :], in0=acc_tiles[b][:], in1=b3_all[:], op=ALU.add
             )
 
+        def head_abs(b):
+            n = halves(b)
+            abs_z = head_pool.tile([P, 2, C], F32, name="abs_z")
+            nc.vector.scalar_tensor_tensor(
+                out=abs_z[:, :n, :], in0=logits[:, b, :n, :], scalar=-1.0, in1=logits[:, b, :n, :],
+                op0=ALU.mult, op1=ALU.max,
+            )
+            abs_tiles[b] = abs_z
+
         def head_log_term(b):
-            nc.scalar.activation(out=sig_z[:, b, :], in_=abs_z[:, b, :], func=ACT.Sigmoid)
-            nc.scalar.activation(out=ln_sig[:, b, :], in_=sig_z[:, b, :], func=ACT.Ln)
+            n = halves(b)
+            sig_z = head_pool.tile([P, 2, C], F32, name="sig_z")
+            ln_sig = head_pool.tile([P, 2, C], F32, name="ln_sig")
+            nc.scalar.activation(out=sig_z[:, :n, :], in_=abs_tiles[b][:, :n, :], func=ACT.Sigmoid)
+            nc.scalar.activation(out=ln_sig[:, :n, :], in_=sig_z[:, :n, :], func=ACT.Ln)
+            ln_sig_tiles[b] = ln_sig
 
         def head_evidence(b):
             one = slice(b, b + 1)
+            n = halves(b)
             nc.vector.scalar_tensor_tensor(
-                out=evidence[:, b, :], in0=logits[:, b, :], scalar=0.0, in1=ln_sig[:, b, :],
+                out=evidence[:, b, :n, :], in0=logits[:, b, :n, :], scalar=0.0,
+                in1=ln_sig_tiles[b][:, :n, :],
                 op0=ALU.max, op1=ALU.subtract, accum_out=sum_e[:, one],
             )
             nc.vector.tensor_scalar(
-                out=c_eps[:, one], in0=sum_e[:, one], scalar1=float(C), scalar2=EPS_B,
+                out=c_eps[:, one], in0=sum_e[:, one], scalar1=float(n * C), scalar2=EPS_B / n,
                 op0=ALU.add, op1=ALU.mult,
             )
+            if b == 0:
+                nc.scalar.activation(
+                    out=ln_e0[:], in_=evidence[:, b, 0:1, :].to_broadcast([P, 2, C]),
+                    func=ACT.Ln, bias=TINY,
+                )
+            else:
+                nc.scalar.activation(
+                    out=ln_e[:, b, :], in_=evidence[:, b, 1, :], func=ACT.Ln, bias=TINY
+                )
             nc.scalar.activation(
-                out=ln_e2[:, b, :, :],
-                in_=evidence[:, b, :].unsqueeze(1).to_broadcast([P, 2, C]),
-                func=ACT.Ln,
-                bias=TINY,
+                out=ln_ec[:, b, :], in_=evidence[:, b, n - 1, :], func=ACT.Ln, bias=c_eps[:, one]
             )
-            nc.scalar.activation(
-                out=ln_ec[:, b, :], in_=evidence[:, b, :], func=ACT.Ln, bias=c_eps[:, one]
-            )
+            nc.vector.tensor_scalar_mul(out=neg_ln_ec[:, b, :], in0=ln_ec[:, b, :], scalar1=-1.0)
 
         def head_pair_operands(b):
             one = slice(b, b + 1)
-            nc.vector.tensor_scalar_add(out=strength[:, one], in0=sum_e[:, one], scalar1=float(C))
+            n = halves(b)
+            e = evidence[:, b, n - 1, :]
+            nc.vector.tensor_scalar(
+                out=strength[:, one], in0=sum_e[:, one], scalar1=1.0 / n, scalar2=float(C),
+                op0=ALU.mult, op1=ALU.add,
+            )
             nc.vector.reciprocal(out=inv_s[:, one], in_=strength[:, one])
             nc.vector.tensor_scalar_mul(out=half_c[:, one], in0=c_eps[:, one], scalar1=0.5)
-            nc.vector.tensor_scalar_mul(
-                out=belief[:, b, :], in0=evidence[:, b, :], scalar1=inv_s[:, one]
-            )
+            nc.vector.tensor_scalar_mul(out=belief[:, b, :], in0=e, scalar1=inv_s[:, one])
             nc.vector.tensor_scalar(
                 out=belief_h2[:, b, :, :],
-                in0=evidence[:, b, :].unsqueeze(1).to_broadcast([P, 2, C]),
+                in0=e.unsqueeze(1).to_broadcast([P, 2, C]),
                 scalar1=half_c[:, one], scalar2=inv_s[:, one], op0=ALU.add, op1=ALU.mult,
             )
             nc.vector.tensor_tensor(
                 out=cap[:, b, :], in0=belief[:, b, :], in1=belief_h2[:, b, 0, :], op=ALU.mult
             )
-            nc.vector.tensor_scalar_mul(out=neg_ln_ec[:, b, :], in0=ln_ec[:, b, :], scalar1=-1.0)
 
         def head_outputs(b):
             one = slice(b, b + 1)
-            nc.vector.tensor_scalar_add(out=alpha[:, b, :], in0=evidence[:, b, :], scalar1=1.0)
+            nc.vector.tensor_scalar_add(out=alpha[:, b, :], in0=evidence[:, b, 0, :], scalar1=1.0)
             nc.vector.tensor_scalar_mul(out=prob[:, b, :], in0=alpha[:, b, :], scalar1=inv_s[:, one])
             nc.vector.tensor_scalar_mul(out=per_row[:, one], in0=inv_s[:, one], scalar1=float(C))
 
         def run_length(c):
             return HALF if c * CHUNK_I < HALF else HALF - 1
 
-        def ratio_chunk(k):
-            b, c = divmod(k, CHUNKS_PER_BLOCK)
+        def ratio(i):
+            c, ii = divmod(i, CHUNK_I)
             n = run_length(c)
-            logs = ln_e2[:, b, :, :].rearrange("p d c -> p (d c)")
-            ratio = pair_pool.tile([P, CHUNK_I * HALF], F32, name="ratio")
-            ratio_tiles[k] = ratio
-            for ii in range(CHUNK_I):
-                i = c * CHUNK_I + ii
-                nc.scalar.activation(
-                    out=ratio[:, ii * n : (ii + 1) * n],
-                    in_=logs[:, i + 1 : i + 1 + n],
-                    func=ACT.Sigmoid,
-                    bias=neg_ln_ec[:, b, i : i + 1],
-                )
+            if ii == 0:
+                tile_c = ratio_pool.tile([P, CHUNK_I * HALF], F32, name="tile_c")
+                ratio_tiles[c] = tile_c
+            nc.scalar.activation(
+                out=ratio_tiles[c][:, ii * n : (ii + 1) * n],
+                in_=ln_e0[:].rearrange("p d c -> p (d c)")[:, i + 1 : i + 1 + n],
+                func=ACT.Sigmoid,
+                bias=neg_ln_ec[:, 0, i : i + 1],
+            )
 
-        def weight_chunk(k):
-            b, c = divmod(k, CHUNKS_PER_BLOCK)
-            n = run_length(c)
-            partners = belief_h2[:, b, :, :].rearrange("p d c -> p (d c)")
-            weight = pair_pool.tile([P, CHUNK_I * HALF], F32, name="weight")
-            weight_tiles[k] = weight
-            for ii in range(CHUNK_I):
-                i = c * CHUNK_I + ii
+        def weights(i0, i1):
+            partners = belief_h2[:, 0, :, :].rearrange("p d c -> p (d c)")
+            for i in range(i0, i1):
+                c, ii = divmod(i, CHUNK_I)
+                n = run_length(c)
+                if ii == 0:
+                    weight = weight_pool.tile([P, CHUNK_I * HALF], F32, name="weight")
+                    weight_tiles[c] = weight
                 nc.vector.tensor_scalar(
-                    out=weight[:, ii * n : (ii + 1) * n],
+                    out=weight_tiles[c][:, ii * n : (ii + 1) * n],
                     in0=partners[:, i + 1 : i + 1 + n],
-                    scalar1=belief[:, b, i : i + 1],
-                    scalar2=cap[:, b, i : i + 1],
+                    scalar1=belief[:, 0, i : i + 1],
+                    scalar2=cap[:, 0, i : i + 1],
                     op0=ALU.mult,
                     op1=ALU.min,
                 )
 
-        def sum_chunk(k):
-            b, c = divmod(k, CHUNKS_PER_BLOCK)
+        def sum_chunk(c):
             used = slice(0, CHUNK_I * run_length(c))
-            weight = weight_tiles[k]
             nc.vector.scalar_tensor_tensor(
-                out=weight[:, used], in0=weight[:, used], scalar=2.0, in1=ratio_tiles[k][:, used],
-                op0=ALU.mult, op1=ALU.mult, accum_out=part[:, b, c : c + 1],
+                out=weight_tiles[c][:, used], in0=weight_tiles[c][:, used], scalar=2.0,
+                in1=ratio_tiles[c][:, used],
+                op0=ALU.mult, op1=ALU.mult, accum_out=part[:, c : c + 1],
+            )
+
+        def sorted_pairs(b):
+            for j in range(1, C):
+                place = (j % 16) * C
+                nc.scalar.activation(
+                    out=unused[:, place : place + j],
+                    in_=ln_e[:, b, 0:j],
+                    func=ACT.Sigmoid,
+                    bias=neg_ln_ec[:, b, j : j + 1],
+                    accum_out=above[:, b, j : j + 1],
+                )
+
+        def sorted_dissonance(b):
+            nc.vector.scalar_tensor_tensor(
+                out=cap[:, b, :], in0=cap[:, b, :], scalar=2.0, in1=above[:, b, :],
+                op0=ALU.mult, op1=ALU.mult, accum_out=per_row[:, BLOCKS + b : BLOCKS + b + 1],
             )
 
         nc.vector.memset(w_planes[:].bitcast(I32), 0)
         make_identity(nc, ident[:])
         nc.gpsimd.memset(per_row[:], 0.0)
+        nc.gpsimd.memset(above[:], 0.0)
         nc.gpsimd.memset(warm[:], 0.0)
         nc.scalar.activation(out=warm[:, 1:2], in_=warm[:, 0:1], func=ACT.Sigmoid)
         for f in range(STEPS_PER_BLOCK):
@@ -300,48 +456,83 @@ def tile_evidentialhead_pb_k_kernel(
 
         block_banks = STEPS_PER_BLOCK * STEP_BANKS
         for f in range(STEPS_PER_BLOCK):
-            evacuate_step(f, vector_banks=2, refill_end=block_banks)
-            quantise_step(f)
+            for j in range(STEP_BANKS):
+                copy_bank(f * STEP_BANKS + j, "vector" if j == 0 else "scalar", block_banks)
+            quantise(f, 0, STEP_GROUPS)
+            if f == STEPS_PER_BLOCK - 2:
+                for early in range(f):
+                    multiply(early, 0, STEP_GROUPS)
+            if f >= STEPS_PER_BLOCK - 2:
+                multiply(f, 0, STEP_GROUPS)
         for n in range(block_banks, block_banks + BANKS_AHEAD):
             transpose_bank(n)
-        head_logits(0)
-        head_log_term(0)
-        head_evidence(0)
-        head_pair_operands(0)
-        head_outputs(0)
-        evacuate_step(STEPS_PER_BLOCK, vector_banks=STEP_BANKS)
-        for f in range(STEPS_PER_BLOCK + 1, FIRST_STEPS):
-            quantise_step(f - 1)
-            evacuate_step(f, vector_banks=STEP_BANKS)
 
-        copied = FIRST_STEPS
-        for k in range(CHUNKS):
-            next_block = (k + 1) // CHUNKS_PER_BLOCK
-            with_head = (k + 1) % CHUNKS_PER_BLOCK == 0 and next_block < BLOCKS
-            if with_head:
-                head_logits(next_block)
-            ratio_chunk(k)
-            if with_head:
-                head_log_term(next_block)
-            weight_chunk(k)
-            for f in range(copied, min(k + FE_LEAD, STEPS) + 1):
-                quantise_step(f - 1)
-                if f < STEPS:
-                    evacuate_step(f, vector_banks=0)
-            copied = max(copied, min(k + FE_LEAD, STEPS) + 1)
-            if k > 0:
-                sum_chunk(k - 1)
-            if with_head:
-                head_evidence(next_block)
-                head_pair_operands(next_block)
-                head_outputs(next_block)
-        sum_chunk(CHUNKS - 1)
+        head_logits(0)
+        head_abs(0)
+        head_log_term(0)
+        copy_bank(block_banks, "vector")
+        copy_bank(block_banks + 1, "scalar")
+        head_evidence(0)
+
+        done = 0
+        for f in range(STEPS_PER_BLOCK, 2 * STEPS_PER_BLOCK):
+            for j in range(STEP_BANKS):
+                n = f * STEP_BANKS + j
+                if n < block_banks + 2:
+                    continue
+                if j % 2 == 0:
+                    copy_bank(n, "vector")
+                else:
+                    copy_bank(n, "scalar")
+                    for i in range(done, done + RATIOS_PER_COPY):
+                        ratio(i)
+                    done += RATIOS_PER_COPY
+            if f > STEPS_PER_BLOCK:
+                quantise(f - 1, 0, STEP_GROUPS)
+                multiply(f - 1, 0, STEP_GROUPS)
+        for i in range(done, C):
+            ratio(i)
+        quantise(2 * STEPS_PER_BLOCK - 1, 0, STEP_GROUPS)
+        multiply(2 * STEPS_PER_BLOCK - 1, 0, STEP_GROUPS)
+
+        for b in range(1, BLOCKS):
+            head_logits(b)
+            if b == 1:
+                head_pair_operands(0)
+                head_outputs(0)
+            if b + 1 < BLOCKS:
+                pieces = vector_front_end(b + 1)
+            else:
+                pieces = [partial(weights, i, i + 4) for i in range(0, CHUNK_I * 2, 4)]
+            for k, step in enumerate(sort_steps(b)):
+                step()
+                if k < len(pieces):
+                    pieces[k]()
+            head_abs(b)
+            head_log_term(b)
+            for piece in pieces[28:30]:
+                piece()
+            head_evidence(b)
+            sorted_pairs(b)
+            for piece in pieces[30:]:
+                piece()
+            head_pair_operands(b)
+            head_outputs(b)
+        sum_chunk(0)
+        sum_chunk(1)
+        for c in range(2, CHUNKS):
+            weights(c * CHUNK_I, (c + 1) * CHUNK_I)
+            sum_chunk(c)
+        for b in range(1, BLOCKS):
+            sorted_dissonance(b)
         nc.sync.dma_start(out=out_0.rearrange("(b p) c -> p b c", p=P), in_=alpha[:])
-        nc.sync.dma_start(out=out_1.rearrange("(b p) c -> p b c", p=P), in_=evidence[:])
+        nc.sync.dma_start(
+            out=out_1.rearrange("(b p) c -> p b c", p=P), in_=evidence[:, :, 0, :]
+        )
         nc.sync.dma_start(out=out_2.rearrange("(b p) c -> p b c", p=P), in_=prob[:])
 
         nc.vector.tensor_reduce(
-            out=per_row[:, BLOCKS : 2 * BLOCKS], in_=part[:], axis=AX.X, op=ALU.add
+            out=per_row[:, BLOCKS : BLOCKS + 1], in_=part[:], axis=AX.X, op=ALU.add
         )
         turned = psum_t.tile([P, P], F32, name="turned", tag="xt")
         nc.tensor.transpose(turned[:], per_row[:], ident[:])

@@ -42,10 +42,20 @@ W_PIECES = 4
 HALF = C // 2
 CHUNK_I = 32
 CHUNKS = C // CHUNK_I
-RATIOS_PER_COPY = 5
-RANKS = 4
-LANE = C // RANKS
-
+RATIO_BUFS = 5
+SORTED = 1
+SLOTS = BLOCKS + 1
+LANES = 4
+RATIOS_PER_COPY = 2
+RATIOS_BEFORE = 112
+FIRST_PIECES = 4
+ROW_CHUNKS = 8
+HEAD_CUT = 4
+PIECES_OF_STEP = 3
+LEFT_FOR_HEAD = 12
+CHUNKS_UNBROKEN = 0
+VECTOR_BANKS = [(0,) if f < 10 else () for f in range(16)]
+FIRST_RANKS = 14
 
 def tile_evidentialhead_pb_k_kernel(
     tc, h_act, W3_words, W3_scales, b3, out_0, out_1, out_2, out_3, out_4
@@ -58,9 +68,8 @@ def tile_evidentialhead_pb_k_kernel(
         h_pool = stack.enter_context(tc.tile_pool(name="h", bufs=H_BUFS))
         grouped_pool = stack.enter_context(tc.tile_pool(name="grouped", bufs=3))
         codes_pool = stack.enter_context(tc.tile_pool(name="codes", bufs=2))
-        ratio_pool = stack.enter_context(tc.tile_pool(name="ratio", bufs=CHUNKS))
+        ratio_pool = stack.enter_context(tc.tile_pool(name="ratio", bufs=RATIO_BUFS))
         weight_pool = stack.enter_context(tc.tile_pool(name="weight", bufs=2))
-        head_pool = stack.enter_context(tc.tile_pool(name="head", bufs=2))
         sort_pool = stack.enter_context(tc.tile_pool(name="sort", bufs=4))
         psum_t = stack.enter_context(tc.psum_pool(name="psum_t", bufs=BANKS_AHEAD))
         psum_acc = stack.enter_context(tc.psum_pool(name="psum_acc", bufs=2))
@@ -71,26 +80,28 @@ def tile_evidentialhead_pb_k_kernel(
         w_words = const.tile([P, GROUPS, 2 * C], U8, name="w_words", align_bytes=64)
         w_planes = const.tile([P, GROUPS, C], U8, name="w_planes", align_bytes=64)
         b3_all = const.tile([P, C], BF16, name="b3_all")
-        unused = const.tile([P, 16 * C], F32, name="unused")
+        first_rows = const.tile([P, FIRST_RANKS, C], F32, name="first_rows")
 
-        logits = const.tile([P, BLOCKS, 2, C], F32, name="logits")
-        evidence = const.tile([P, BLOCKS, 2, C], F32, name="evidence")
+        logits = const.tile([P, SLOTS, C], F32, name="logits")
+        abs_z = const.tile([P, SLOTS, C], F32, name="abs_z")
+        relu_z = const.tile([P, SLOTS, C], F32, name="relu_z")
+        ln_sig = const.tile([P, SLOTS, C], F32, name="ln_sig")
+        evidence = const.tile([P, SLOTS, C], F32, name="evidence")
         alpha = const.tile([P, BLOCKS, C], F32, name="alpha")
         prob = const.tile([P, BLOCKS, C], F32, name="prob")
-        ln_e0 = const.tile([P, 2, C], F32, name="ln_e0")
-        ln_e = const.tile([P, BLOCKS, C], F32, name="ln_e")
-        ln_ec = const.tile([P, BLOCKS, C], F32, name="ln_ec")
-        neg_ln_ec = const.tile([P, BLOCKS, C], F32, name="neg_ln_ec")
-        belief = const.tile([P, BLOCKS, C], F32, name="belief")
-        belief_h2 = const.tile([P, BLOCKS, 2, C], F32, name="belief_h2")
-        cap = const.tile([P, BLOCKS, C], F32, name="cap")
-        above = const.tile([P, BLOCKS, C], F32, name="above")
-        sum_e = const.tile([P, BLOCKS], F32, name="sum_e")
-        c_eps = const.tile([P, BLOCKS], F32, name="c_eps")
-        half_c = const.tile([P, BLOCKS], F32, name="half_c")
-        strength = const.tile([P, BLOCKS], F32, name="strength")
-        inv_s = const.tile([P, BLOCKS], F32, name="inv_s")
-        part = const.tile([P, CHUNKS], F32, name="part")
+        ln_e2 = const.tile([P, SLOTS, 2, C], F32, name="ln_e2")
+        ln_ec = const.tile([P, SLOTS, C], F32, name="ln_ec")
+        neg_ln_ec = const.tile([P, SLOTS, C], F32, name="neg_ln_ec")
+        belief = const.tile([P, SLOTS, C], F32, name="belief")
+        belief_h2 = const.tile([P, SLOTS, 2, C], F32, name="belief_h2")
+        cap = const.tile([P, SLOTS, C], F32, name="cap")
+        above = const.tile([P, C], F32, name="above")
+        sum_e = const.tile([P, SLOTS], F32, name="sum_e")
+        c_eps = const.tile([P, SLOTS], F32, name="c_eps")
+        half_c = const.tile([P, SLOTS], F32, name="half_c")
+        strength = const.tile([P, SLOTS], F32, name="strength")
+        inv_s = const.tile([P, SLOTS], F32, name="inv_s")
+        part = const.tile([P, BLOCKS, CHUNKS], F32, name="part")
         per_row = const.tile([P, P], F32, name="per_row")
         per_row_t = const.tile([P, P], F32, name="per_row_t")
 
@@ -99,15 +110,20 @@ def tile_evidentialhead_pb_k_kernel(
         grouped_tiles = {}
         code_tiles = {}
         acc_tiles = {}
-        abs_tiles = {}
-        ln_sig_tiles = {}
         ratio_tiles = {}
         weight_tiles = {}
+        rows = {}
 
         def load_chunk(f):
             b, q = divmod(f, STEPS_PER_BLOCK)
-            h_chunk = h_pool.tile([P, STEP_K], BF16, name="h_chunk")
-            nc.sync.dma_start(out=h_chunk[:], in_=h_rows[:, b, q * STEP_K : (q + 1) * STEP_K])
+            h_chunk = h_pool.tile([P, STEP_K], BF16, name="h_chunk", tag="h_chunk")
+            pieces = FIRST_PIECES if f == 0 else 1
+            width = STEP_K // pieces
+            for k in range(0, STEP_K, width):
+                nc.sync.dma_start(
+                    out=h_chunk[:, k : k + width],
+                    in_=h_rows[:, b, q * STEP_K + k : q * STEP_K + k + width],
+                )
             chunks[f] = h_chunk
 
         def load_weights():
@@ -165,14 +181,6 @@ def tile_evidentialhead_pb_k_kernel(
                 nc.vector.tensor_copy(out=dst, in_=src)
             bank_done(n, refill_end)
 
-        def copy_half_bank(n, g):
-            f, j = divmod(n, STEP_BANKS)
-            nc.vector.tensor_copy(
-                out=grouped_view(f)[:, j, g], in_=banks[n][:, g].rearrange("p u r -> p r u")
-            )
-            if g == BANK_GROUPS - 1:
-                bank_done(n, BANKS)
-
         def quantise(f, g0, g1):
             b, q = divmod(f, STEPS_PER_BLOCK)
             if q == 0 and g0 == 0:
@@ -205,33 +213,15 @@ def tile_evidentialhead_pb_k_kernel(
                     stop=(g == GROUPS - 1),
                 )
 
-        def vector_front_end(b):
-            half = STEP_GROUPS // 2
-            pieces = []
-
-            def quantise_half(f, g0):
-                quantise(f, g0, g0 + half)
-                multiply(f, g0, g0 + half)
-
-            for f in range(b * STEPS_PER_BLOCK, (b + 1) * STEPS_PER_BLOCK):
-                for j in range(STEP_BANKS):
-                    for g in range(BANK_GROUPS):
-                        pieces.append(partial(copy_half_bank, f * STEP_BANKS + j, g))
-                        if f > b * STEPS_PER_BLOCK and j < 2 and g == 1:
-                            pieces.append(partial(quantise_half, f - 1, j * half))
-            for g0 in (0, half):
-                pieces.append(partial(quantise_half, (b + 1) * STEPS_PER_BLOCK - 1, g0))
-            return pieces
-
-        def sort_steps(b):
+        def sort_steps():
             steps = []
-            state = {"src": logits[:, b, 0, :]}
+            state = {"src": logits[:, SORTED, :]}
 
             def compare(hi0, hi1, pick, last=False):
                 def step():
                     src = state["src"]
                     if last:
-                        dst = logits[:, b, 1, :]
+                        dst = logits[:, BLOCKS, :]
                     else:
                         buf = sort_pool.tile([P, C], F32, name="buf")
                         dst = buf[:]
@@ -262,7 +252,7 @@ def tile_evidentialhead_pb_k_kernel(
             )
             for top in range(2, 7):
                 m = 2 ** (top - 2)
-                lanes = dict(q=RANKS, t=2, m=m)
+                lanes = dict(q=LANES, t=2, m=m)
                 compare(
                     lambda s, lanes=lanes: s.rearrange(
                         "p (q h t m) -> p h t m q", **lanes
@@ -305,145 +295,166 @@ def tile_evidentialhead_pb_k_kernel(
                     )
             return steps
 
-        def halves(b):
-            return 1 if b == 0 else 2
-
         def head_logits(b):
             nc.vector.tensor_tensor(
-                out=logits[:, b, 0, :], in0=acc_tiles[b][:], in1=b3_all[:], op=ALU.add
+                out=logits[:, b, :], in0=acc_tiles[b][:], in1=b3_all[:], op=ALU.add
             )
 
-        def head_abs(b):
-            n = halves(b)
-            abs_z = head_pool.tile([P, 2, C], F32, name="abs_z")
-            nc.vector.scalar_tensor_tensor(
-                out=abs_z[:, :n, :], in0=logits[:, b, :n, :], scalar=-1.0, in1=logits[:, b, :n, :],
-                op0=ALU.mult, op1=ALU.max,
+        def head_softplus(s0, s1):
+            z = logits[:, s0:s1, :]
+            nc.gpsimd.tensor_scalar(
+                out=relu_z[:, s0:s1, :], in0=z, scalar1=0.0, scalar2=0.0, op0=ALU.max, op1=ALU.add
             )
-            abs_tiles[b] = abs_z
+            nc.scalar.activation(out=abs_z[:, s0:s1, :], in_=z, func=ACT.Abs)
+            nc.scalar.activation(out=abs_z[:, s0:s1, :], in_=abs_z[:, s0:s1, :], func=ACT.Sigmoid)
+            nc.scalar.activation(out=ln_sig[:, s0:s1, :], in_=abs_z[:, s0:s1, :], func=ACT.Ln)
+            nc.gpsimd.tensor_tensor(
+                out=evidence[:, s0:s1, :], in0=relu_z[:, s0:s1, :], in1=ln_sig[:, s0:s1, :],
+                op=ALU.subtract,
+            )
 
-        def head_log_term(b):
-            n = halves(b)
-            sig_z = head_pool.tile([P, 2, C], F32, name="sig_z")
-            ln_sig = head_pool.tile([P, 2, C], F32, name="ln_sig")
-            nc.scalar.activation(out=sig_z[:, :n, :], in_=abs_tiles[b][:, :n, :], func=ACT.Sigmoid)
-            nc.scalar.activation(out=ln_sig[:, :n, :], in_=sig_z[:, :n, :], func=ACT.Ln)
-            ln_sig_tiles[b] = ln_sig
-
-        def head_evidence(b):
-            one = slice(b, b + 1)
-            n = halves(b)
-            nc.vector.scalar_tensor_tensor(
-                out=evidence[:, b, :n, :], in0=logits[:, b, :n, :], scalar=0.0,
-                in1=ln_sig_tiles[b][:, :n, :],
-                op0=ALU.max, op1=ALU.subtract, accum_out=sum_e[:, one],
-            )
-            nc.vector.tensor_scalar(
-                out=c_eps[:, one], in0=sum_e[:, one], scalar1=float(n * C), scalar2=EPS_B / n,
-                op0=ALU.add, op1=ALU.mult,
-            )
-            if b == 0:
+        def head_logs(s0, s1, pairs):
+            for s in pairs:
+                copies = 2 if s < BLOCKS else 1
                 nc.scalar.activation(
-                    out=ln_e0[:], in_=evidence[:, b, 0:1, :].to_broadcast([P, 2, C]),
-                    func=ACT.Ln, bias=TINY,
+                    out=ln_e2[:, s, :copies, :],
+                    in_=evidence[:, s : s + 1, :].to_broadcast([P, copies, C]),
+                    func=ACT.Ln,
+                    bias=TINY,
                 )
-            else:
+            for s in range(s0, s1):
                 nc.scalar.activation(
-                    out=ln_e[:, b, :], in_=evidence[:, b, 1, :], func=ACT.Ln, bias=TINY
+                    out=abs_z[:, s, :], in_=evidence[:, s, :], func=ACT.Copy,
+                    accum_out=sum_e[:, s : s + 1],
                 )
             nc.scalar.activation(
-                out=ln_ec[:, b, :], in_=evidence[:, b, n - 1, :], func=ACT.Ln, bias=c_eps[:, one]
+                out=c_eps[:, s0:s1], in_=sum_e[:, s0:s1], func=ACT.Copy, scale=EPS_B, bias=C * EPS_B
             )
-            nc.vector.tensor_scalar_mul(out=neg_ln_ec[:, b, :], in0=ln_ec[:, b, :], scalar1=-1.0)
+            for s in pairs:
+                nc.scalar.activation(
+                    out=ln_ec[:, s, :], in_=evidence[:, s, :], func=ACT.Ln, bias=c_eps[:, s : s + 1]
+                )
+                if s < BLOCKS:
+                    nc.scalar.activation(
+                        out=neg_ln_ec[:, s, :], in_=ln_ec[:, s, :], func=ACT.Copy, scale=-1.0
+                    )
 
-        def head_pair_operands(b):
-            one = slice(b, b + 1)
-            n = halves(b)
-            e = evidence[:, b, n - 1, :]
-            nc.vector.tensor_scalar(
-                out=strength[:, one], in0=sum_e[:, one], scalar1=1.0 / n, scalar2=float(C),
-                op0=ALU.mult, op1=ALU.add,
+        def head_scales(s0, s1):
+            some = slice(s0, s1)
+            nc.vector.tensor_scalar_add(out=strength[:, some], in0=sum_e[:, some], scalar1=float(C))
+            nc.vector.reciprocal(out=inv_s[:, some], in_=strength[:, some])
+            nc.vector.tensor_scalar_mul(out=half_c[:, some], in0=c_eps[:, some], scalar1=0.5)
+
+        def head_pair_operands(s):
+            one = slice(s, s + 1)
+            nc.vector.tensor_scalar_mul(
+                out=belief[:, s, :], in0=evidence[:, s, :], scalar1=inv_s[:, one]
             )
-            nc.vector.reciprocal(out=inv_s[:, one], in_=strength[:, one])
-            nc.vector.tensor_scalar_mul(out=half_c[:, one], in0=c_eps[:, one], scalar1=0.5)
-            nc.vector.tensor_scalar_mul(out=belief[:, b, :], in0=e, scalar1=inv_s[:, one])
             nc.vector.tensor_scalar(
-                out=belief_h2[:, b, :, :],
-                in0=e.unsqueeze(1).to_broadcast([P, 2, C]),
+                out=belief_h2[:, s, :, :],
+                in0=evidence[:, one, :].to_broadcast([P, 2, C]),
                 scalar1=half_c[:, one], scalar2=inv_s[:, one], op0=ALU.add, op1=ALU.mult,
             )
             nc.vector.tensor_tensor(
-                out=cap[:, b, :], in0=belief[:, b, :], in1=belief_h2[:, b, 0, :], op=ALU.mult
+                out=cap[:, s, :], in0=belief[:, s, :], in1=belief_h2[:, s, 0, :], op=ALU.mult
             )
 
         def head_outputs(b):
             one = slice(b, b + 1)
-            nc.vector.tensor_scalar_add(out=alpha[:, b, :], in0=evidence[:, b, 0, :], scalar1=1.0)
+            nc.vector.tensor_scalar_add(out=alpha[:, b, :], in0=evidence[:, b, :], scalar1=1.0)
             nc.vector.tensor_scalar_mul(out=prob[:, b, :], in0=alpha[:, b, :], scalar1=inv_s[:, one])
             nc.vector.tensor_scalar_mul(out=per_row[:, one], in0=inv_s[:, one], scalar1=float(C))
 
         def run_length(c):
             return HALF if c * CHUNK_I < HALF else HALF - 1
 
-        def ratio(i):
+        def ratio(b, i):
             c, ii = divmod(i, CHUNK_I)
             n = run_length(c)
             if ii == 0:
-                tile_c = ratio_pool.tile([P, CHUNK_I * HALF], F32, name="tile_c")
-                ratio_tiles[c] = tile_c
+                ratios = ratio_pool.tile([P, CHUNK_I * HALF], F32, name="ratios")
+                ratio_tiles[b, c] = ratios
             nc.scalar.activation(
-                out=ratio_tiles[c][:, ii * n : (ii + 1) * n],
-                in_=ln_e0[:].rearrange("p d c -> p (d c)")[:, i + 1 : i + 1 + n],
+                out=ratio_tiles[b, c][:, ii * n : (ii + 1) * n],
+                in_=ln_e2[:, b, :, :].rearrange("p d c -> p (d c)")[:, i + 1 : i + 1 + n],
                 func=ACT.Sigmoid,
-                bias=neg_ln_ec[:, 0, i : i + 1],
+                bias=neg_ln_ec[:, b, i : i + 1],
             )
 
-        def weights(i0, i1):
-            partners = belief_h2[:, 0, :, :].rearrange("p d c -> p (d c)")
+        def weights(b, i0, i1):
+            partners = belief_h2[:, b, :, :].rearrange("p d c -> p (d c)")
             for i in range(i0, i1):
                 c, ii = divmod(i, CHUNK_I)
                 n = run_length(c)
                 if ii == 0:
                     weight = weight_pool.tile([P, CHUNK_I * HALF], F32, name="weight")
-                    weight_tiles[c] = weight
+                    weight_tiles[b, c] = weight
                 nc.vector.tensor_scalar(
-                    out=weight_tiles[c][:, ii * n : (ii + 1) * n],
+                    out=weight_tiles[b, c][:, ii * n : (ii + 1) * n],
                     in0=partners[:, i + 1 : i + 1 + n],
-                    scalar1=belief[:, 0, i : i + 1],
-                    scalar2=cap[:, 0, i : i + 1],
+                    scalar1=belief[:, b, i : i + 1],
+                    scalar2=cap[:, b, i : i + 1],
                     op0=ALU.mult,
                     op1=ALU.min,
                 )
 
-        def sum_chunk(c):
+        def sum_chunk(b, c):
             used = slice(0, CHUNK_I * run_length(c))
+            weight = weight_tiles[b, c]
             nc.vector.scalar_tensor_tensor(
-                out=weight_tiles[c][:, used], in0=weight_tiles[c][:, used], scalar=2.0,
-                in1=ratio_tiles[c][:, used],
-                op0=ALU.mult, op1=ALU.mult, accum_out=part[:, c : c + 1],
+                out=weight[:, used], in0=weight[:, used], scalar=2.0,
+                in1=ratio_tiles[b, c][:, used],
+                op0=ALU.mult, op1=ALU.mult, accum_out=part[:, b, c : c + 1],
             )
 
-        def sorted_pairs(b):
-            for j in range(1, C):
-                place = (j % 16) * C
-                nc.scalar.activation(
-                    out=unused[:, place : place + j],
-                    in_=ln_e[:, b, 0:j],
-                    func=ACT.Sigmoid,
-                    bias=neg_ln_ec[:, b, j : j + 1],
-                    accum_out=above[:, b, j : j + 1],
+        def sorted_row(i):
+            n = C - 1 - i
+            if i < FIRST_RANKS:
+                row = first_rows[:, i, i + 1 : C]
+            else:
+                if "tile" not in rows or rows["used"] + n > STEP_K // 2:
+                    row_tile = h_pool.tile([P, STEP_K // 2], F32, name="row_tile", tag="h_chunk")
+                    rows["tile"] = row_tile
+                    rows["used"] = 0
+                row = rows["tile"][:, rows["used"] : rows["used"] + n]
+                rows["used"] += n
+            nc.scalar.activation(
+                out=row,
+                in_=ln_ec[:, BLOCKS, i + 1 : C],
+                func=ACT.Sigmoid,
+                scale=-1.0,
+                bias=ln_e2[:, BLOCKS, 0, i : i + 1],
+            )
+            if i == FIRST_RANKS:
+                above_acc = psum_acc.tile([P, C], F32, name="acc")
+                rows["acc"] = above_acc
+            if i >= FIRST_RANKS:
+                nc.tensor.matmul(
+                    rows["acc"][:, i + 1 : C],
+                    lhsT=ident[:],
+                    rhs=row,
+                    start=(i == FIRST_RANKS),
+                    stop=(i == C - 2),
                 )
 
-        def sorted_dissonance(b):
+        def sorted_dissonance():
+            nc.vector.tensor_reduce(
+                out=above[:], in_=first_rows[:].rearrange("p i j -> p j i"), axis=AX.X, op=ALU.add
+            )
+            n = FIRST_RANKS + 1
+            nc.vector.tensor_tensor(
+                out=above[:, n:C], in0=rows["acc"][:, n:C], in1=above[:, n:C], op=ALU.add
+            )
             nc.vector.scalar_tensor_tensor(
-                out=cap[:, b, :], in0=cap[:, b, :], scalar=2.0, in1=above[:, b, :],
-                op0=ALU.mult, op1=ALU.mult, accum_out=per_row[:, BLOCKS + b : BLOCKS + b + 1],
+                out=cap[:, BLOCKS, :], in0=cap[:, BLOCKS, :], scalar=2.0, in1=above[:],
+                op0=ALU.mult, op1=ALU.mult, accum_out=part[:, SORTED, 0:1],
             )
 
         nc.vector.memset(w_planes[:].bitcast(I32), 0)
         make_identity(nc, ident[:])
         nc.gpsimd.memset(per_row[:], 0.0)
-        nc.gpsimd.memset(above[:], 0.0)
+        nc.gpsimd.memset(first_rows[:], 0.0)
+        nc.gpsimd.memset(part[:], 0.0)
         nc.gpsimd.memset(warm[:], 0.0)
         nc.scalar.activation(out=warm[:, 1:2], in_=warm[:, 0:1], func=ACT.Sigmoid)
         for f in range(STEPS_PER_BLOCK):
@@ -468,71 +479,99 @@ def tile_evidentialhead_pb_k_kernel(
             transpose_bank(n)
 
         head_logits(0)
-        head_abs(0)
-        head_log_term(0)
+        head_softplus(0, 1)
         copy_bank(block_banks, "vector")
         copy_bank(block_banks + 1, "scalar")
-        head_evidence(0)
+        head_logs(0, 1, (0,))
+        head_scales(0, 1)
 
-        done = 0
-        for f in range(STEPS_PER_BLOCK, 2 * STEPS_PER_BLOCK):
+        half = STEP_GROUPS // 2
+        sort_from = (SORTED + 1) * STEPS_PER_BLOCK + 1
+        sort_queue = sort_steps()
+        sort_ready = [False]
+
+        def woven(pieces):
+            for piece in pieces:
+                if sort_queue and sort_ready[0]:
+                    sort_queue.pop(0)()
+                piece()
+
+        pair_queue = []
+        for c in range(CHUNKS):
+            first = c * CHUNK_I
+            pair_queue += [partial(weights, 0, i, i + 4) for i in range(first, first + CHUNK_I, 4)]
+            pair_queue.append(partial(sum_chunk, 0, c))
+        pair_pieces = CHUNK_I // 4 + 1
+        pieces_done = 0
+        ratios_done = 0
+        for f in range(STEPS_PER_BLOCK, STEPS):
             for j in range(STEP_BANKS):
                 n = f * STEP_BANKS + j
-                if n < block_banks + 2:
-                    continue
-                if j % 2 == 0:
-                    copy_bank(n, "vector")
-                else:
-                    copy_bank(n, "scalar")
-                    for i in range(done, done + RATIOS_PER_COPY):
-                        ratio(i)
-                    done += RATIOS_PER_COPY
-            if f > STEPS_PER_BLOCK:
-                quantise(f - 1, 0, STEP_GROUPS)
-                multiply(f - 1, 0, STEP_GROUPS)
-        for i in range(done, C):
-            ratio(i)
-        quantise(2 * STEPS_PER_BLOCK - 1, 0, STEP_GROUPS)
-        multiply(2 * STEPS_PER_BLOCK - 1, 0, STEP_GROUPS)
+                if n >= block_banks + 2:
+                    copy_bank(n, "vector" if j in VECTOR_BANKS[f] else "scalar")
+                    more = min(ratios_done + RATIOS_PER_COPY, RATIOS_BEFORE)
+                    for i in range(ratios_done, more):
+                        ratio(0, i)
+                    ratios_done = more
+                if j == 1 and f > STEPS_PER_BLOCK:
+                    if f == sort_from:
+                        head_logits(SORTED)
+                        sort_ready[0] = True
+                    woven([partial(quantise, f - 1, g0, g0 + half) for g0 in (0, half)])
+                    multiply(f - 1, 0, STEP_GROUPS)
+                if j == 3:
+                    if f == STEPS_PER_BLOCK:
+                        head_pair_operands(0)
+                    room = (ratios_done // CHUNK_I + 1) * pair_pieces - 1
+                    more = min(pieces_done + PIECES_OF_STEP, room)
+                    woven(pair_queue[pieces_done:more])
+                    pieces_done = max(more, pieces_done)
+        woven([partial(quantise, STEPS - 1, g0, g0 + half) for g0 in (0, half)])
+        multiply(STEPS - 1, 0, STEP_GROUPS)
+        for i in range(ratios_done, C):
+            ratio(0, i)
+        left = pair_queue[pieces_done:]
+        spare = max(0, len(left) - LEFT_FOR_HEAD)
+        woven(left[:spare])
+        left = left[spare:]
+        head_logits(2)
+        for step in sort_queue:
+            step()
 
-        for b in range(1, BLOCKS):
-            head_logits(b)
-            if b == 1:
-                head_pair_operands(0)
-                head_outputs(0)
-            if b + 1 < BLOCKS:
-                pieces = vector_front_end(b + 1)
-            else:
-                pieces = [partial(weights, i, i + 4) for i in range(0, CHUNK_I * 2, 4)]
-            for k, step in enumerate(sort_steps(b)):
-                step()
-                if k < len(pieces):
-                    pieces[k]()
-            head_abs(b)
-            head_log_term(b)
-            for piece in pieces[28:30]:
-                piece()
-            head_evidence(b)
-            sorted_pairs(b)
-            for piece in pieces[30:]:
-                piece()
-            head_pair_operands(b)
+        cut = HEAD_CUT
+        head_logits(3)
+        head_softplus(1, SLOTS)
+        for piece in left[:cut]:
+            piece()
+        head_logs(1, SLOTS, (2, 3, BLOCKS))
+        for piece in left[cut:]:
+            piece()
+        head_scales(1, SLOTS)
+        for s in (2, 3, BLOCKS):
+            head_pair_operands(s)
+        for b in range(BLOCKS):
             head_outputs(b)
-        sum_chunk(0)
-        sum_chunk(1)
-        for c in range(2, CHUNKS):
-            weights(c * CHUNK_I, (c + 1) * CHUNK_I)
-            sum_chunk(c)
-        for b in range(1, BLOCKS):
-            sorted_dissonance(b)
         nc.sync.dma_start(out=out_0.rearrange("(b p) c -> p b c", p=P), in_=alpha[:])
         nc.sync.dma_start(
-            out=out_1.rearrange("(b p) c -> p b c", p=P), in_=evidence[:, :, 0, :]
+            out=out_1.rearrange("(b p) c -> p b c", p=P), in_=evidence[:, :BLOCKS, :]
         )
         nc.sync.dma_start(out=out_2.rearrange("(b p) c -> p b c", p=P), in_=prob[:])
+        order = [(2, c) for c in range(CHUNKS)] + [(3, c) for c in range(CHUNKS)]
+        done = 0
+        for k, (b, c) in enumerate(order):
+            for i in range(c * CHUNK_I, (c + 1) * CHUNK_I):
+                ratio(b, i)
+            if k >= CHUNKS_UNBROKEN:
+                more = min(C - 1, (C - 1) * (k - CHUNKS_UNBROKEN + 1) // ROW_CHUNKS)
+                for i in range(done, more):
+                    sorted_row(i)
+                done = more
+            weights(b, c * CHUNK_I, (c + 1) * CHUNK_I)
+            sum_chunk(b, c)
+        sorted_dissonance()
 
         nc.vector.tensor_reduce(
-            out=per_row[:, BLOCKS : BLOCKS + 1], in_=part[:], axis=AX.X, op=ALU.add
+            out=per_row[:, BLOCKS : 2 * BLOCKS], in_=part[:], axis=AX.X, op=ALU.add
         )
         turned = psum_t.tile([P, P], F32, name="turned", tag="xt")
         nc.tensor.transpose(turned[:], per_row[:], ident[:])

@@ -43,19 +43,18 @@ HALF = C // 2
 CHUNK_I = 32
 CHUNKS = C // CHUNK_I
 RATIO_BUFS = 5
-SORTED = 1
-SLOTS = BLOCKS + 1
+SLOT = (0, 1, 2, 3)
+SORTED = {1: 4}
+SLOTS = 5
+RATIOS_PER_COPY = 3
+RATIOS_BESIDE = 96
 LANES = 4
-RATIOS_PER_COPY = 2
-RATIOS_BEFORE = 112
 FIRST_PIECES = 4
-ROW_CHUNKS = 8
-HEAD_CUT = 4
-PIECES_OF_STEP = 3
-LEFT_FOR_HEAD = 12
-CHUNKS_UNBROKEN = 0
 VECTOR_BANKS = [(0,) if f < 10 else () for f in range(16)]
-FIRST_RANKS = 14
+ROW_CHUNKS = 6
+FIRST_RANKS = 15
+ROWS_OF_PASS = 4
+ROWS_OF_TILE = 16
 
 def tile_evidentialhead_pb_k_kernel(
     tc, h_act, W3_words, W3_scales, b3, out_0, out_1, out_2, out_3, out_4
@@ -73,7 +72,15 @@ def tile_evidentialhead_pb_k_kernel(
         sort_pool = stack.enter_context(tc.tile_pool(name="sort", bufs=4))
         psum_t = stack.enter_context(tc.psum_pool(name="psum_t", bufs=BANKS_AHEAD))
         psum_acc = stack.enter_context(tc.psum_pool(name="psum_acc", bufs=2))
-        stack.enter_context(tc.manual_schedule())
+        stack.enter_context(
+            tc.manual_schedule(
+                engines={
+                    mybir.EngineType.SP,
+                    mybir.EngineType.Activation,
+                    mybir.EngineType.Pool,
+                }
+            )
+        )
 
         ident = const.tile([P, P], F32, name="ident")
         warm = const.tile([P, 2], F32, name="warm")
@@ -84,7 +91,6 @@ def tile_evidentialhead_pb_k_kernel(
 
         logits = const.tile([P, SLOTS, C], F32, name="logits")
         abs_z = const.tile([P, SLOTS, C], F32, name="abs_z")
-        relu_z = const.tile([P, SLOTS, C], F32, name="relu_z")
         ln_sig = const.tile([P, SLOTS, C], F32, name="ln_sig")
         evidence = const.tile([P, SLOTS, C], F32, name="evidence")
         alpha = const.tile([P, BLOCKS, C], F32, name="alpha")
@@ -95,10 +101,9 @@ def tile_evidentialhead_pb_k_kernel(
         belief = const.tile([P, SLOTS, C], F32, name="belief")
         belief_h2 = const.tile([P, SLOTS, 2, C], F32, name="belief_h2")
         cap = const.tile([P, SLOTS, C], F32, name="cap")
-        above = const.tile([P, C], F32, name="above")
+        above = const.tile([P, 2, C], F32, name="above")
         sum_e = const.tile([P, SLOTS], F32, name="sum_e")
         c_eps = const.tile([P, SLOTS], F32, name="c_eps")
-        half_c = const.tile([P, SLOTS], F32, name="half_c")
         strength = const.tile([P, SLOTS], F32, name="strength")
         inv_s = const.tile([P, SLOTS], F32, name="inv_s")
         part = const.tile([P, BLOCKS, CHUNKS], F32, name="part")
@@ -198,7 +203,7 @@ def tile_evidentialhead_pb_k_kernel(
         def multiply(f, g0, g1):
             b, q = divmod(f, STEPS_PER_BLOCK)
             if q == 0 and g0 == 0:
-                acc = psum_acc.tile([P, C], F32, name="acc")
+                acc = psum_acc.tile([P, C], F32, name="acc", tag="acc")
                 acc_tiles[b] = acc
             h_codes, h_scales = code_tiles[b]
             for g in range(q * STEP_GROUPS + g0, q * STEP_GROUPS + g1):
@@ -213,15 +218,15 @@ def tile_evidentialhead_pb_k_kernel(
                     stop=(g == GROUPS - 1),
                 )
 
-        def sort_steps():
+        def sort_steps(b):
             steps = []
-            state = {"src": logits[:, SORTED, :]}
+            state = {"src": logits[:, SLOT[b], :]}
 
             def compare(hi0, hi1, pick, last=False):
                 def step():
                     src = state["src"]
                     if last:
-                        dst = logits[:, BLOCKS, :]
+                        dst = logits[:, SORTED[b], :]
                     else:
                         buf = sort_pool.tile([P, C], F32, name="buf")
                         dst = buf[:]
@@ -297,73 +302,68 @@ def tile_evidentialhead_pb_k_kernel(
 
         def head_logits(b):
             nc.vector.tensor_tensor(
-                out=logits[:, b, :], in0=acc_tiles[b][:], in1=b3_all[:], op=ALU.add
+                out=logits[:, SLOT[b], :], in0=acc_tiles[b][:], in1=b3_all[:], op=ALU.add
             )
 
-        def head_softplus(s0, s1):
-            z = logits[:, s0:s1, :]
-            nc.gpsimd.tensor_scalar(
-                out=relu_z[:, s0:s1, :], in0=z, scalar1=0.0, scalar2=0.0, op0=ALU.max, op1=ALU.add
+        def head_abs(s):
+            nc.vector.scalar_tensor_tensor(
+                out=abs_z[:, s, :], in0=logits[:, s, :], scalar=-1.0, in1=logits[:, s, :],
+                op0=ALU.mult, op1=ALU.max,
             )
-            nc.scalar.activation(out=abs_z[:, s0:s1, :], in_=z, func=ACT.Abs)
+
+        def head(s0, s1, pairs):
             nc.scalar.activation(out=abs_z[:, s0:s1, :], in_=abs_z[:, s0:s1, :], func=ACT.Sigmoid)
             nc.scalar.activation(out=ln_sig[:, s0:s1, :], in_=abs_z[:, s0:s1, :], func=ACT.Ln)
-            nc.gpsimd.tensor_tensor(
-                out=evidence[:, s0:s1, :], in0=relu_z[:, s0:s1, :], in1=ln_sig[:, s0:s1, :],
-                op=ALU.subtract,
-            )
-
-        def head_logs(s0, s1, pairs):
+            order = list(pairs) + [s for s in range(s0, s1) if s not in pairs]
+            for s in order:
+                nc.vector.scalar_tensor_tensor(
+                    out=evidence[:, s, :], in0=logits[:, s, :], scalar=0.0, in1=ln_sig[:, s, :],
+                    op0=ALU.max, op1=ALU.subtract, accum_out=sum_e[:, s : s + 1],
+                )
             for s in pairs:
-                copies = 2 if s < BLOCKS else 1
+                one = slice(s, s + 1)
+                nc.vector.tensor_scalar(
+                    out=c_eps[:, one], in0=sum_e[:, one], scalar1=float(C), scalar2=EPS_B,
+                    op0=ALU.add, op1=ALU.mult,
+                )
+                copies = 1 if s in SORTED.values() else 2
                 nc.scalar.activation(
                     out=ln_e2[:, s, :copies, :],
-                    in_=evidence[:, s : s + 1, :].to_broadcast([P, copies, C]),
+                    in_=evidence[:, one, :].to_broadcast([P, copies, C]),
                     func=ACT.Ln,
                     bias=TINY,
                 )
-            for s in range(s0, s1):
                 nc.scalar.activation(
-                    out=abs_z[:, s, :], in_=evidence[:, s, :], func=ACT.Copy,
-                    accum_out=sum_e[:, s : s + 1],
+                    out=ln_ec[:, s, :], in_=evidence[:, s, :], func=ACT.Ln, bias=c_eps[:, one]
                 )
-            nc.scalar.activation(
-                out=c_eps[:, s0:s1], in_=sum_e[:, s0:s1], func=ACT.Copy, scale=EPS_B, bias=C * EPS_B
-            )
-            for s in pairs:
-                nc.scalar.activation(
-                    out=ln_ec[:, s, :], in_=evidence[:, s, :], func=ACT.Ln, bias=c_eps[:, s : s + 1]
+                nc.vector.tensor_scalar_mul(
+                    out=neg_ln_ec[:, s, :], in0=ln_ec[:, s, :], scalar1=-1.0
                 )
-                if s < BLOCKS:
-                    nc.scalar.activation(
-                        out=neg_ln_ec[:, s, :], in_=ln_ec[:, s, :], func=ACT.Copy, scale=-1.0
-                    )
-
-        def head_scales(s0, s1):
             some = slice(s0, s1)
             nc.vector.tensor_scalar_add(out=strength[:, some], in0=sum_e[:, some], scalar1=float(C))
             nc.vector.reciprocal(out=inv_s[:, some], in_=strength[:, some])
-            nc.vector.tensor_scalar_mul(out=half_c[:, some], in0=c_eps[:, some], scalar1=0.5)
-
-        def head_pair_operands(s):
-            one = slice(s, s + 1)
-            nc.vector.tensor_scalar_mul(
-                out=belief[:, s, :], in0=evidence[:, s, :], scalar1=inv_s[:, one]
-            )
-            nc.vector.tensor_scalar(
-                out=belief_h2[:, s, :, :],
-                in0=evidence[:, one, :].to_broadcast([P, 2, C]),
-                scalar1=half_c[:, one], scalar2=inv_s[:, one], op0=ALU.add, op1=ALU.mult,
-            )
-            nc.vector.tensor_tensor(
-                out=cap[:, s, :], in0=belief[:, s, :], in1=belief_h2[:, s, 0, :], op=ALU.mult
-            )
+            for s in pairs:
+                one = slice(s, s + 1)
+                nc.vector.tensor_scalar_mul(
+                    out=belief[:, s, :], in0=evidence[:, s, :], scalar1=inv_s[:, one]
+                )
+                nc.vector.tensor_scalar(
+                    out=belief_h2[:, s, :, :],
+                    in0=evidence[:, one, :].to_broadcast([P, 2, C]),
+                    scalar1=inv_s[:, one], scalar2=EPS_B / 2, op0=ALU.mult, op1=ALU.add,
+                )
+                nc.vector.tensor_tensor(
+                    out=cap[:, s, :], in0=belief[:, s, :], in1=belief_h2[:, s, 0, :], op=ALU.mult
+                )
 
         def head_outputs(b):
-            one = slice(b, b + 1)
-            nc.vector.tensor_scalar_add(out=alpha[:, b, :], in0=evidence[:, b, :], scalar1=1.0)
+            s = SLOT[b]
+            one = slice(s, s + 1)
+            nc.vector.tensor_scalar_add(out=alpha[:, b, :], in0=evidence[:, s, :], scalar1=1.0)
             nc.vector.tensor_scalar_mul(out=prob[:, b, :], in0=alpha[:, b, :], scalar1=inv_s[:, one])
-            nc.vector.tensor_scalar_mul(out=per_row[:, one], in0=inv_s[:, one], scalar1=float(C))
+            nc.vector.tensor_scalar_mul(
+                out=per_row[:, b : b + 1], in0=inv_s[:, one], scalar1=float(C)
+            )
 
         def run_length(c):
             return HALF if c * CHUNK_I < HALF else HALF - 1
@@ -376,13 +376,13 @@ def tile_evidentialhead_pb_k_kernel(
                 ratio_tiles[b, c] = ratios
             nc.scalar.activation(
                 out=ratio_tiles[b, c][:, ii * n : (ii + 1) * n],
-                in_=ln_e2[:, b, :, :].rearrange("p d c -> p (d c)")[:, i + 1 : i + 1 + n],
+                in_=ln_e2[:, SLOT[b], :, :].rearrange("p d c -> p (d c)")[:, i + 1 : i + 1 + n],
                 func=ACT.Sigmoid,
-                bias=neg_ln_ec[:, b, i : i + 1],
+                bias=neg_ln_ec[:, SLOT[b], i : i + 1],
             )
 
         def weights(b, i0, i1):
-            partners = belief_h2[:, b, :, :].rearrange("p d c -> p (d c)")
+            partners = belief_h2[:, SLOT[b], :, :].rearrange("p d c -> p (d c)")
             for i in range(i0, i1):
                 c, ii = divmod(i, CHUNK_I)
                 n = run_length(c)
@@ -392,8 +392,8 @@ def tile_evidentialhead_pb_k_kernel(
                 nc.vector.tensor_scalar(
                     out=weight_tiles[b, c][:, ii * n : (ii + 1) * n],
                     in0=partners[:, i + 1 : i + 1 + n],
-                    scalar1=belief[:, b, i : i + 1],
-                    scalar2=cap[:, b, i : i + 1],
+                    scalar1=belief[:, SLOT[b], i : i + 1],
+                    scalar2=cap[:, SLOT[b], i : i + 1],
                     op0=ALU.mult,
                     op1=ALU.min,
                 )
@@ -408,46 +408,56 @@ def tile_evidentialhead_pb_k_kernel(
             )
 
         def sorted_row(i):
-            n = C - 1 - i
             if i < FIRST_RANKS:
                 row = first_rows[:, i, i + 1 : C]
             else:
-                if "tile" not in rows or rows["used"] + n > STEP_K // 2:
-                    row_tile = h_pool.tile([P, STEP_K // 2], F32, name="row_tile", tag="h_chunk")
+                k, r = divmod(i - FIRST_RANKS, ROWS_OF_PASS)
+                if (i - FIRST_RANKS) % ROWS_OF_TILE == 0:
+                    row_tile = h_pool.tile([P, ROWS_OF_TILE, C], F32, name="row_tile", tag="h_chunk")
                     rows["tile"] = row_tile
-                    rows["used"] = 0
-                row = rows["tile"][:, rows["used"] : rows["used"] + n]
-                rows["used"] += n
-            nc.scalar.activation(
-                out=row,
-                in_=ln_ec[:, BLOCKS, i + 1 : C],
-                func=ACT.Sigmoid,
-                scale=-1.0,
-                bias=ln_e2[:, BLOCKS, 0, i : i + 1],
-            )
+                at = (i - FIRST_RANKS) % ROWS_OF_TILE
+                if r == 0:
+                    nc.gpsimd.memset(
+                        rows["tile"][:, at : at + ROWS_OF_PASS, i + 1 : i + ROWS_OF_PASS], 0.0
+                    )
+                row = rows["tile"][:, at, i + 1 : C]
+            if i + 1 < C:
+                nc.scalar.activation(
+                    out=row,
+                    in_=ln_ec[:, SORTED[1], i + 1 : C],
+                    func=ACT.Sigmoid,
+                    scale=-1.0,
+                    bias=ln_e2[:, SORTED[1], 0, i : i + 1],
+                )
             if i == FIRST_RANKS:
-                above_acc = psum_acc.tile([P, C], F32, name="acc")
+                above_acc = psum_acc.tile([P, ROWS_OF_PASS, C], F32, name="above_acc", tag="acc")
                 rows["acc"] = above_acc
-            if i >= FIRST_RANKS:
+            if i >= FIRST_RANKS and r == ROWS_OF_PASS - 1:
+                first = i - r
                 nc.tensor.matmul(
-                    rows["acc"][:, i + 1 : C],
+                    rows["acc"][:, :, first + 1 : C],
                     lhsT=ident[:],
-                    rhs=row,
-                    start=(i == FIRST_RANKS),
-                    stop=(i == C - 2),
+                    rhs=rows["tile"][:, at - r : at + 1, first + 1 : C],
+                    start=(first == FIRST_RANKS),
+                    stop=(first == C - 1 - ROWS_OF_PASS),
                 )
 
         def sorted_dissonance():
-            nc.vector.tensor_reduce(
-                out=above[:], in_=first_rows[:].rearrange("p i j -> p j i"), axis=AX.X, op=ALU.add
-            )
             n = FIRST_RANKS + 1
+            nc.vector.tensor_reduce(
+                out=above[:, 0, :], in_=first_rows[:].rearrange("p i j -> p j i"), axis=AX.X,
+                op=ALU.add,
+            )
+            nc.vector.tensor_reduce(
+                out=above[:, 1, n:C], in_=rows["acc"][:, :, n:C].rearrange("p r j -> p j r"),
+                axis=AX.X, op=ALU.add,
+            )
             nc.vector.tensor_tensor(
-                out=above[:, n:C], in0=rows["acc"][:, n:C], in1=above[:, n:C], op=ALU.add
+                out=above[:, 0, n:C], in0=above[:, 0, n:C], in1=above[:, 1, n:C], op=ALU.add
             )
             nc.vector.scalar_tensor_tensor(
-                out=cap[:, BLOCKS, :], in0=cap[:, BLOCKS, :], scalar=2.0, in1=above[:],
-                op0=ALU.mult, op1=ALU.mult, accum_out=part[:, SORTED, 0:1],
+                out=cap[:, SORTED[1], :], in0=cap[:, SORTED[1], :], scalar=2.0, in1=above[:, 0, :],
+                op0=ALU.mult, op1=ALU.mult, accum_out=part[:, 1, 0:1],
             )
 
         nc.vector.memset(w_planes[:].bitcast(I32), 0)
@@ -478,77 +488,44 @@ def tile_evidentialhead_pb_k_kernel(
         for n in range(block_banks, block_banks + BANKS_AHEAD):
             transpose_bank(n)
 
-        head_logits(0)
-        head_softplus(0, 1)
-        copy_bank(block_banks, "vector")
-        copy_bank(block_banks + 1, "scalar")
-        head_logs(0, 1, (0,))
-        head_scales(0, 1)
+        def logits_done(b):
+            head_logits(b)
+            head_abs(SLOT[b])
+            if b in SORTED:
+                for step in sort_steps(b):
+                    step()
+                head_abs(SORTED[b])
 
-        half = STEP_GROUPS // 2
-        sort_from = (SORTED + 1) * STEPS_PER_BLOCK + 1
-        sort_queue = sort_steps()
-        sort_ready = [False]
+        logits_done(0)
+        head(0, 1, (0,))
 
-        def woven(pieces):
-            for piece in pieces:
-                if sort_queue and sort_ready[0]:
-                    sort_queue.pop(0)()
-                piece()
-
-        pair_queue = []
-        for c in range(CHUNKS):
-            first = c * CHUNK_I
-            pair_queue += [partial(weights, 0, i, i + 4) for i in range(first, first + CHUNK_I, 4)]
-            pair_queue.append(partial(sum_chunk, 0, c))
-        pair_pieces = CHUNK_I // 4 + 1
-        pieces_done = 0
         ratios_done = 0
         for f in range(STEPS_PER_BLOCK, STEPS):
-            for j in range(STEP_BANKS):
-                n = f * STEP_BANKS + j
-                if n >= block_banks + 2:
-                    copy_bank(n, "vector" if j in VECTOR_BANKS[f] else "scalar")
-                    more = min(ratios_done + RATIOS_PER_COPY, RATIOS_BEFORE)
+            for jb in range(STEP_BANKS):
+                by_vector = jb in VECTOR_BANKS[f]
+                copy_bank(f * STEP_BANKS + jb, "vector" if by_vector else "scalar")
+                if not by_vector:
+                    more = min(ratios_done + RATIOS_PER_COPY, RATIOS_BESIDE)
                     for i in range(ratios_done, more):
                         ratio(0, i)
                     ratios_done = more
-                if j == 1 and f > STEPS_PER_BLOCK:
-                    if f == sort_from:
-                        head_logits(SORTED)
-                        sort_ready[0] = True
-                    woven([partial(quantise, f - 1, g0, g0 + half) for g0 in (0, half)])
+                if jb == 1 and f > STEPS_PER_BLOCK:
+                    quantise(f - 1, 0, STEP_GROUPS)
                     multiply(f - 1, 0, STEP_GROUPS)
-                if j == 3:
-                    if f == STEPS_PER_BLOCK:
-                        head_pair_operands(0)
-                    room = (ratios_done // CHUNK_I + 1) * pair_pieces - 1
-                    more = min(pieces_done + PIECES_OF_STEP, room)
-                    woven(pair_queue[pieces_done:more])
-                    pieces_done = max(more, pieces_done)
-        woven([partial(quantise, STEPS - 1, g0, g0 + half) for g0 in (0, half)])
-        multiply(STEPS - 1, 0, STEP_GROUPS)
+                    b, q = divmod(f - 1, STEPS_PER_BLOCK)
+                    if q == STEPS_PER_BLOCK - 1:
+                        logits_done(b)
+        for g0 in (0, STEP_GROUPS // 2):
+            quantise(STEPS - 1, g0, g0 + STEP_GROUPS // 2)
+            multiply(STEPS - 1, g0, g0 + STEP_GROUPS // 2)
+        logits_done(BLOCKS - 1)
         for i in range(ratios_done, C):
             ratio(0, i)
-        left = pair_queue[pieces_done:]
-        spare = max(0, len(left) - LEFT_FOR_HEAD)
-        woven(left[:spare])
-        left = left[spare:]
-        head_logits(2)
-        for step in sort_queue:
-            step()
 
-        cut = HEAD_CUT
-        head_logits(3)
-        head_softplus(1, SLOTS)
-        for piece in left[:cut]:
-            piece()
-        head_logs(1, SLOTS, (2, 3, BLOCKS))
-        for piece in left[cut:]:
-            piece()
-        head_scales(1, SLOTS)
-        for s in (2, 3, BLOCKS):
-            head_pair_operands(s)
+        head(1, SLOTS, (2, 4, 3))
+        for c in range(CHUNKS):
+            weights(0, c * CHUNK_I, (c + 1) * CHUNK_I)
+            sum_chunk(0, c)
         for b in range(BLOCKS):
             head_outputs(b)
         nc.sync.dma_start(out=out_0.rearrange("(b p) c -> p b c", p=P), in_=alpha[:])
@@ -556,18 +533,18 @@ def tile_evidentialhead_pb_k_kernel(
             out=out_1.rearrange("(b p) c -> p b c", p=P), in_=evidence[:, :BLOCKS, :]
         )
         nc.sync.dma_start(out=out_2.rearrange("(b p) c -> p b c", p=P), in_=prob[:])
-        order = [(2, c) for c in range(CHUNKS)] + [(3, c) for c in range(CHUNKS)]
+
         done = 0
-        for k, (b, c) in enumerate(order):
+        for k in range(2 * CHUNKS):
+            b, c = divmod(k, CHUNKS)
             for i in range(c * CHUNK_I, (c + 1) * CHUNK_I):
-                ratio(b, i)
-            if k >= CHUNKS_UNBROKEN:
-                more = min(C - 1, (C - 1) * (k - CHUNKS_UNBROKEN + 1) // ROW_CHUNKS)
-                for i in range(done, more):
-                    sorted_row(i)
-                done = more
-            weights(b, c * CHUNK_I, (c + 1) * CHUNK_I)
-            sum_chunk(b, c)
+                ratio(2 + b, i)
+            more = min(C - 1, (C - 1) * (k + 1) // ROW_CHUNKS)
+            for i in range(done, more):
+                sorted_row(i)
+            done = more
+            weights(2 + b, c * CHUNK_I, (c + 1) * CHUNK_I)
+            sum_chunk(2 + b, c)
         sorted_dissonance()
 
         nc.vector.tensor_reduce(

@@ -51,6 +51,8 @@ RATIOS_BESIDE = 96
 LANES = 4
 FIRST_PIECES = 4
 VECTOR_BANKS = [(0,) if f < 10 else () for f in range(16)]
+QUANTISE_GROUPS = 2
+SUM_PARTS = 8
 ROW_CHUNKS = 6
 FIRST_RANKS = 15
 ROWS_OF_PASS = 4
@@ -106,7 +108,7 @@ def tile_evidentialhead_pb_k_kernel(
         c_eps = const.tile([P, SLOTS], F32, name="c_eps")
         strength = const.tile([P, SLOTS], F32, name="strength")
         inv_s = const.tile([P, SLOTS], F32, name="inv_s")
-        part = const.tile([P, BLOCKS, CHUNKS], F32, name="part")
+        part = const.tile([P, BLOCKS, CHUNKS * SUM_PARTS], F32, name="part")
         per_row = const.tile([P, P], F32, name="per_row")
         per_row_t = const.tile([P, P], F32, name="per_row_t")
 
@@ -399,13 +401,17 @@ def tile_evidentialhead_pb_k_kernel(
                 )
 
         def sum_chunk(b, c):
-            used = slice(0, CHUNK_I * run_length(c))
             weight = weight_tiles[b, c]
-            nc.vector.scalar_tensor_tensor(
-                out=weight[:, used], in0=weight[:, used], scalar=2.0,
-                in1=ratio_tiles[b, c][:, used],
-                op0=ALU.mult, op1=ALU.mult, accum_out=part[:, b, c : c + 1],
-            )
+            parts = SUM_PARTS if b == 0 else 1
+            width = CHUNK_I * run_length(c) // parts
+            for k in range(parts):
+                used = slice(k * width, (k + 1) * width)
+                at = c * SUM_PARTS + k
+                nc.vector.scalar_tensor_tensor(
+                    out=weight[:, used], in0=weight[:, used], scalar=2.0,
+                    in1=ratio_tiles[b, c][:, used],
+                    op0=ALU.mult, op1=ALU.mult, accum_out=part[:, b, at : at + 1],
+                )
 
         def sorted_row(i):
             if i < FIRST_RANKS:
@@ -510,7 +516,8 @@ def tile_evidentialhead_pb_k_kernel(
                         ratio(0, i)
                     ratios_done = more
                 if jb == 1 and f > STEPS_PER_BLOCK:
-                    quantise(f - 1, 0, STEP_GROUPS)
+                    for g0 in range(0, STEP_GROUPS, QUANTISE_GROUPS):
+                        quantise(f - 1, g0, g0 + QUANTISE_GROUPS)
                     multiply(f - 1, 0, STEP_GROUPS)
                     b, q = divmod(f - 1, STEPS_PER_BLOCK)
                     if q == STEPS_PER_BLOCK - 1:

@@ -46,14 +46,18 @@ RATIO_BUFS = 5
 SLOT = (0, 1, 2, 3)
 SORTED = {1: 4}
 SLOTS = 5
-RATIOS_PER_COPY = 3
-RATIOS_BESIDE = 96
+RATIOS_PER_COPY = 2
+RATIOS_BESIDE = 112
 LANES = 4
 FIRST_PIECES = 4
-VECTOR_BANKS = [(0,) if f < 10 else () for f in range(16)]
+VECTOR_BANKS = [(0,) if f < 7 else () for f in range(16)]
 QUANTISE_GROUPS = 2
+LAST_PARTS = 4
+LONG_PARTS = 2
+DIFF_LEAD = 2
+DIFF_CHUNKS = (3, 5)
 SUM_PARTS = 8
-ROW_CHUNKS = 6
+ROW_CHUNKS = 8
 FIRST_RANKS = 15
 ROWS_OF_PASS = 4
 ROWS_OF_TILE = 16
@@ -78,6 +82,7 @@ def tile_evidentialhead_pb_k_kernel(
             tc.manual_schedule(
                 engines={
                     mybir.EngineType.SP,
+                    mybir.EngineType.PE,
                     mybir.EngineType.Activation,
                     mybir.EngineType.Pool,
                 }
@@ -374,7 +379,7 @@ def tile_evidentialhead_pb_k_kernel(
             c, ii = divmod(i, CHUNK_I)
             n = run_length(c)
             if ii == 0:
-                ratios = ratio_pool.tile([P, CHUNK_I * HALF], F32, name="ratios")
+                ratios = ratio_pool.tile([P, CHUNK_I * HALF], F32, name="ratios", tag="ratios")
                 ratio_tiles[b, c] = ratios
             nc.scalar.activation(
                 out=ratio_tiles[b, c][:, ii * n : (ii + 1) * n],
@@ -382,6 +387,25 @@ def tile_evidentialhead_pb_k_kernel(
                 func=ACT.Sigmoid,
                 bias=neg_ln_ec[:, SLOT[b], i : i + 1],
             )
+
+        def differences(b, c):
+            n = run_length(c)
+            ratio_tile = ratio_pool.tile([P, CHUNK_I * HALF], F32, name="ratios", tag="ratios")
+            ratio_tiles[b, c] = ratio_tile
+            logs = ln_e2[:, SLOT[b], :, :].rearrange("p d c -> p (d c)")
+            for ii in range(CHUNK_I):
+                i = c * CHUNK_I + ii
+                nc.vector.tensor_scalar_add(
+                    out=ratio_tile[:, ii * n : (ii + 1) * n],
+                    in0=logs[:, i + 1 : i + 1 + n],
+                    scalar1=neg_ln_ec[:, SLOT[b], i : i + 1],
+                )
+
+        def long_ratio(b, c):
+            for k in range(LONG_PARTS):
+                width = CHUNK_I * run_length(c) // LONG_PARTS
+                used = ratio_tiles[b, c][:, k * width : (k + 1) * width]
+                nc.scalar.activation(out=used, in_=used, func=ACT.Sigmoid)
 
         def weights(b, i0, i1):
             partners = belief_h2[:, SLOT[b], :, :].rearrange("p d c -> p (d c)")
@@ -402,7 +426,7 @@ def tile_evidentialhead_pb_k_kernel(
 
         def sum_chunk(b, c):
             weight = weight_tiles[b, c]
-            parts = SUM_PARTS if b == 0 else 1
+            parts = SUM_PARTS if b == 0 else LAST_PARTS if (b, c) == (3, CHUNKS - 1) else 1
             width = CHUNK_I * run_length(c) // parts
             for k in range(parts):
                 used = slice(k * width, (k + 1) * width)
@@ -544,8 +568,14 @@ def tile_evidentialhead_pb_k_kernel(
         done = 0
         for k in range(2 * CHUNKS):
             b, c = divmod(k, CHUNKS)
-            for i in range(c * CHUNK_I, (c + 1) * CHUNK_I):
-                ratio(2 + b, i)
+            if k + DIFF_LEAD in DIFF_CHUNKS:
+                b1, c1 = divmod(k + DIFF_LEAD, CHUNKS)
+                differences(2 + b1, c1)
+            if k in DIFF_CHUNKS:
+                long_ratio(2 + b, c)
+            else:
+                for i in range(c * CHUNK_I, (c + 1) * CHUNK_I):
+                    ratio(2 + b, i)
             more = min(C - 1, (C - 1) * (k + 1) // ROW_CHUNKS)
             for i in range(done, more):
                 sorted_row(i)

@@ -46,18 +46,20 @@ RATIO_BUFS = 5
 SLOT = (0, 1, 2, 3)
 SORTED = {1: 4}
 SLOTS = 5
-RATIOS_PER_COPY = 2
-RATIOS_BESIDE = 112
+HEAD_COPIES = 3
+RATIOS_PER_COPY = 3
+RATIOS_BESIDE = 80
 LANES = 4
 FIRST_PIECES = 4
 VECTOR_BANKS = [(0,) if f < 7 else () for f in range(16)]
 QUANTISE_GROUPS = 2
-LAST_PARTS = 4
+LAST_PARTS = 2
 LONG_PARTS = 2
-DIFF_LEAD = 2
-DIFF_CHUNKS = (3, 5)
+DIFF_LEAD = 1
+DIFF_CHUNKS = (2, 4, 6)
 SUM_PARTS = 8
-ROW_CHUNKS = 8
+ROW_CHUNKS = 6
+TILES_BEFORE = 2
 FIRST_RANKS = 15
 ROWS_OF_PASS = 4
 ROWS_OF_TILE = 16
@@ -318,10 +320,15 @@ def tile_evidentialhead_pb_k_kernel(
                 op0=ALU.mult, op1=ALU.max,
             )
 
-        def head(s0, s1, pairs):
+        def head_sigmoid(s0, s1):
             nc.scalar.activation(out=abs_z[:, s0:s1, :], in_=abs_z[:, s0:s1, :], func=ACT.Sigmoid)
-            nc.scalar.activation(out=ln_sig[:, s0:s1, :], in_=abs_z[:, s0:s1, :], func=ACT.Ln)
+
+        def head(s0, s1, pairs, copies_between=0):
             order = list(pairs) + [s for s in range(s0, s1) if s not in pairs]
+            for s in order:
+                nc.scalar.activation(out=ln_sig[:, s, :], in_=abs_z[:, s, :], func=ACT.Ln)
+            for n in range(block_banks + early_banks, block_banks + early_banks + copies_between):
+                copy_bank(n, "scalar")
             for s in order:
                 nc.vector.scalar_tensor_tensor(
                     out=evidence[:, s, :], in0=logits[:, s, :], scalar=0.0, in1=ln_sig[:, s, :],
@@ -340,6 +347,8 @@ def tile_evidentialhead_pb_k_kernel(
                     func=ACT.Ln,
                     bias=TINY,
                 )
+            for s in pairs:
+                one = slice(s, s + 1)
                 nc.scalar.activation(
                     out=ln_ec[:, s, :], in_=evidence[:, s, :], func=ACT.Ln, bias=c_eps[:, one]
                 )
@@ -472,12 +481,14 @@ def tile_evidentialhead_pb_k_kernel(
                     stop=(first == C - 1 - ROWS_OF_PASS),
                 )
 
-        def sorted_dissonance():
-            n = FIRST_RANKS + 1
+        def sum_first_rows():
             nc.vector.tensor_reduce(
                 out=above[:, 0, :], in_=first_rows[:].rearrange("p i j -> p j i"), axis=AX.X,
                 op=ALU.add,
             )
+
+        def sorted_dissonance():
+            n = FIRST_RANKS + 1
             nc.vector.tensor_reduce(
                 out=above[:, 1, n:C], in_=rows["acc"][:, :, n:C].rearrange("p r j -> p j r"),
                 axis=AX.X, op=ALU.add,
@@ -490,6 +501,8 @@ def tile_evidentialhead_pb_k_kernel(
                 op0=ALU.mult, op1=ALU.mult, accum_out=part[:, 1, 0:1],
             )
 
+        block_banks = STEPS_PER_BLOCK * STEP_BANKS
+        early_banks = 0
         nc.vector.memset(w_planes[:].bitcast(I32), 0)
         make_identity(nc, ident[:])
         nc.gpsimd.memset(per_row[:], 0.0)
@@ -526,14 +539,21 @@ def tile_evidentialhead_pb_k_kernel(
                     step()
                 head_abs(SORTED[b])
 
+        early_banks = 0
         logits_done(0)
-        head(0, 1, (0,))
+        head_sigmoid(0, 1)
+        head(0, 1, (0,), HEAD_COPIES)
+        early_banks += HEAD_COPIES
 
         ratios_done = 0
         for f in range(STEPS_PER_BLOCK, STEPS):
             for jb in range(STEP_BANKS):
                 by_vector = jb in VECTOR_BANKS[f]
-                copy_bank(f * STEP_BANKS + jb, "vector" if by_vector else "scalar")
+                n = f * STEP_BANKS + jb
+                if n < block_banks + early_banks:
+                    by_vector = True
+                else:
+                    copy_bank(n, "vector" if by_vector else "scalar")
                 if not by_vector:
                     more = min(ratios_done + RATIOS_PER_COPY, RATIOS_BESIDE)
                     for i in range(ratios_done, more):
@@ -550,9 +570,11 @@ def tile_evidentialhead_pb_k_kernel(
             quantise(STEPS - 1, g0, g0 + STEP_GROUPS // 2)
             multiply(STEPS - 1, g0, g0 + STEP_GROUPS // 2)
         logits_done(BLOCKS - 1)
+        head_sigmoid(1, 3)
         for i in range(ratios_done, C):
             ratio(0, i)
 
+        head_sigmoid(3, SLOTS)
         head(1, SLOTS, (2, 4, 3))
         for c in range(CHUNKS):
             weights(0, c * CHUNK_I, (c + 1) * CHUNK_I)
@@ -565,6 +587,9 @@ def tile_evidentialhead_pb_k_kernel(
         )
         nc.sync.dma_start(out=out_2.rearrange("(b p) c -> p b c", p=P), in_=prob[:])
 
+        later = FIRST_RANKS + ROWS_OF_TILE * TILES_BEFORE
+        row_order = list(range(FIRST_RANKS, later)) + list(range(FIRST_RANKS))
+        row_order += list(range(later, C - 1))
         done = 0
         for k in range(2 * CHUNKS):
             b, c = divmod(k, CHUNKS)
@@ -577,8 +602,10 @@ def tile_evidentialhead_pb_k_kernel(
                 for i in range(c * CHUNK_I, (c + 1) * CHUNK_I):
                     ratio(2 + b, i)
             more = min(C - 1, (C - 1) * (k + 1) // ROW_CHUNKS)
-            for i in range(done, more):
+            for i in row_order[done:more]:
                 sorted_row(i)
+                if i == FIRST_RANKS - 1:
+                    sum_first_rows()
             done = more
             weights(2 + b, c * CHUNK_I, (c + 1) * CHUNK_I)
             sum_chunk(2 + b, c)

@@ -55,9 +55,9 @@ VECTOR_BANKS = [(0,) if f < 7 else () for f in range(16)]
 QUANTISE_GROUPS = 2
 LAST_PARTS = 2
 LONG_PARTS = 2
-DIFF_LEAD = 1
-DIFF_CHUNKS = (2, 4, 6)
-SUM_PARTS = 8
+DIFF_LEAD = 2
+DIFF_CHUNKS = (3, 5)
+SUM_PARTS = 4
 ROW_CHUNKS = 6
 TILES_BEFORE = 2
 FIRST_RANKS = 15
@@ -84,7 +84,6 @@ def tile_evidentialhead_pb_k_kernel(
             tc.manual_schedule(
                 engines={
                     mybir.EngineType.SP,
-                    mybir.EngineType.PE,
                     mybir.EngineType.Activation,
                     mybir.EngineType.Pool,
                 }

from contextlib import ExitStack
from functools import partial

import concourse.mybir as mybir
from concourse.masks import make_identity

F32 = mybir.dt.float32
BF16 = mybir.dt.bfloat16
I32 = mybir.dt.int32
U8 = mybir.dt.uint8
U32 = mybir.dt.uint32
FP8X4 = mybir.dt.float8_e4m3fn_x4
FP4X4 = mybir.dt.float4_e2m1fn_x4
ACT = mybir.ActivationFunctionType
ALU = mybir.AluOpType
AX = mybir.AxisListType

P = 128
ROWS = 512
K_DIM = 16384
C = 128
EPS_B = 1e-8
TINY = 1e-18
FLOPS = 2 * ROWS * K_DIM * C

BLOCKS = ROWS // P
K_PASS = 4 * P
GROUPS = K_DIM // K_PASS
PAIRS_PER_GROUP = K_PASS // 2

STEP_GROUPS = 8
STEP_K = STEP_GROUPS * K_PASS
STEPS_PER_BLOCK = GROUPS // STEP_GROUPS
STEPS = BLOCKS * STEPS_PER_BLOCK
BANK_GROUPS = 2
STEP_BANKS = STEP_GROUPS // BANK_GROUPS
BANKS = STEPS * STEP_BANKS
BANKS_AHEAD = 6
H_BUFS = 7
W_PIECES = 4

HALF = C // 2
CHUNK_I = 32
CHUNKS = C // CHUNK_I
RATIO_BUFS = 5
SLOT = (0, 1, 2, 3)
SORTED = {1: 4}
SLOTS = 5
HEAD_COPIES = 3
RATIOS_PER_COPY = 3
RATIOS_BESIDE = 80
LANES = 4
FIRST_PIECES = 4
VECTOR_BANKS = [(0,) if f < 7 else () for f in range(16)]
QUANTISE_GROUPS = 2
LAST_PARTS = 2
LONG_PARTS = 2
DIFF_LEAD = 2
DIFF_CHUNKS = (3, 5)
SUM_PARTS = 4
ROW_CHUNKS = 6
TILES_BEFORE = 2
FIRST_RANKS = 15
ROWS_OF_PASS = 4
ROWS_OF_TILE = 16

def tile_evidentialhead_pb_k_kernel(
    tc, h_act, W3_words, W3_scales, b3, out_0, out_1, out_2, out_3, out_4
):
    nc = tc.nc
    h_rows = h_act.rearrange("(b p) k -> p b k", p=P)

    with ExitStack() as stack:
        const = stack.enter_context(tc.tile_pool(name="const", bufs=1))
        h_pool = stack.enter_context(tc.tile_pool(name="h", bufs=H_BUFS))
        grouped_pool = stack.enter_context(tc.tile_pool(name="grouped", bufs=3))
        codes_pool = stack.enter_context(tc.tile_pool(name="codes", bufs=2))
        ratio_pool = stack.enter_context(tc.tile_pool(name="ratio", bufs=RATIO_BUFS))
        weight_pool = stack.enter_context(tc.tile_pool(name="weight", bufs=2))
        sort_pool = stack.enter_context(tc.tile_pool(name="sort", bufs=4))
        psum_t = stack.enter_context(tc.psum_pool(name="psum_t", bufs=BANKS_AHEAD))
        psum_acc = stack.enter_context(tc.psum_pool(name="psum_acc", bufs=2))
        stack.enter_context(
            tc.manual_schedule(
                engines={
                    mybir.EngineType.SP,
                    mybir.EngineType.Activation,
                    mybir.EngineType.Pool,
                }
            )
        )

        ident = const.tile([P, P], F32, name="ident")
        warm = const.tile([P, 2], F32, name="warm")
        w_words = const.tile([P, GROUPS, 2 * C], U8, name="w_words", align_bytes=64)
        w_planes = const.tile([P, GROUPS, C], U8, name="w_planes", align_bytes=64)
        b3_all = const.tile([P, C], BF16, name="b3_all")
        first_rows = const.tile([P, FIRST_RANKS, C], F32, name="first_rows")

        logits = const.tile([P, SLOTS, C], F32, name="logits")
        abs_z = const.tile([P, SLOTS, C], F32, name="abs_z")
        ln_sig = const.tile([P, SLOTS, C], F32, name="ln_sig")
        evidence = const.tile([P, SLOTS, C], F32, name="evidence")
        alpha = const.tile([P, BLOCKS, C], F32, name="alpha")
        prob = const.tile([P, BLOCKS, C], F32, name="prob")
        ln_e2 = const.tile([P, SLOTS, 2, C], F32, name="ln_e2")
        ln_ec = const.tile([P, SLOTS, C], F32, name="ln_ec")
        neg_ln_ec = const.tile([P, SLOTS, C], F32, name="neg_ln_ec")
        belief = const.tile([P, SLOTS, C], F32, name="belief")
        belief_h2 = const.tile([P, SLOTS, 2, C], F32, name="belief_h2")
        cap = const.tile([P, SLOTS, C], F32, name="cap")
        above = const.tile([P, 2, C], F32, name="above")
        sum_e = const.tile([P, SLOTS], F32, name="sum_e")
        c_eps = const.tile([P, SLOTS], F32, name="c_eps")
        strength = const.tile([P, SLOTS], F32, name="strength")
        inv_s = const.tile([P, SLOTS], F32, name="inv_s")
        part = const.tile([P, BLOCKS, CHUNKS * SUM_PARTS], F32, name="part")
        per_row = const.tile([P, P], F32, name="per_row")
        per_row_t = const.tile([P, P], F32, name="per_row_t")

        chunks = {}
        banks = {}
        grouped_tiles = {}
        code_tiles = {}
        acc_tiles = {}
        ratio_tiles = {}
        weight_tiles = {}
        rows = {}

        def load_chunk(f):
            b, q = divmod(f, STEPS_PER_BLOCK)
            h_chunk = h_pool.tile([P, STEP_K], BF16, name="h_chunk", tag="h_chunk")
            pieces = FIRST_PIECES if f == 0 else 1
            width = STEP_K // pieces
            for k in range(0, STEP_K, width):
                nc.sync.dma_start(
                    out=h_chunk[:, k : k + width],
                    in_=h_rows[:, b, q * STEP_K + k : q * STEP_K + k + width],
                )
            chunks[f] = h_chunk

        def load_weights():
            scale_words = W3_scales.bitcast(I32)
            for quad in range(4):
                nc.sync.dma_start(
                    out=w_planes[32 * quad : 32 * quad + 4, :, :].bitcast(I32),
                    in_=scale_words[:, 4 * quad : 4 * quad + 4, :].rearrange("g q n -> q g n"),
                )
            words = W3_words.bitcast(I32).rearrange("g p n -> p g n")
            piece = GROUPS // W_PIECES
            for g0 in range(0, GROUPS, piece):
                nc.sync.dma_start(
                    out=w_words[:, g0 : g0 + piece, :].bitcast(I32),
                    in_=words[:, g0 : g0 + piece, :],
                )
            nc.sync.dma_start(out=b3_all[:], in_=b3.partition_broadcast(P))

        def transpose_bank(n):
            f, j = divmod(n, STEP_BANKS)
            pairs = chunks[f][:].bitcast(F32)
            xt = psum_t.tile([P, BANK_GROUPS, 2, P], F32, name="xt")
            for g in range(BANK_GROUPS):
                first = (j * BANK_GROUPS + g) * PAIRS_PER_GROUP
                for u in range(2):
                    nc.tensor.transpose(
                        xt[:, g, u, :],
                        pairs[:, first + u : first + PAIRS_PER_GROUP : 2],
                        ident[:],
                    )
            banks[n] = xt

        def grouped_view(f):
            if f not in grouped_tiles:
                grouped = grouped_pool.tile([P, STEP_K], BF16, name="grouped", align_bytes=64)
                grouped_tiles[f] = grouped
            return grouped_tiles[f][:].bitcast(F32).rearrange(
                "p (j g r u) -> p j g r u", j=STEP_BANKS, g=BANK_GROUPS, u=2
            )

        def bank_done(n, refill_end):
            if n + BANKS_AHEAD < refill_end:
                transpose_bank(n + BANKS_AHEAD)
            f, j = divmod(n, STEP_BANKS)
            if j == STEP_BANKS - 1 and f + H_BUFS < STEPS:
                load_chunk(f + H_BUFS)

        def copy_bank(n, engine, refill_end=BANKS):
            f, j = divmod(n, STEP_BANKS)
            dst = grouped_view(f)[:, j]
            src = banks[n][:].rearrange("p g u r -> p g r u")
            if engine == "scalar":
                nc.scalar.copy(out=dst, in_=src)
            else:
                nc.vector.tensor_copy(out=dst, in_=src)
            bank_done(n, refill_end)

        def quantise(f, g0, g1):
            b, q = divmod(f, STEPS_PER_BLOCK)
            if q == 0 and g0 == 0:
                h_codes = codes_pool.tile([P, GROUPS * P], U32, name="h_codes", align_bytes=64)
                h_scales = codes_pool.tile([P, GROUPS * P], U8, name="h_scales", align_bytes=64)
                code_tiles[b] = (h_codes, h_scales)
            h_codes, h_scales = code_tiles[b]
            cols = slice((q * STEP_GROUPS + g0) * P, (q * STEP_GROUPS + g1) * P)
            nc.vector.quantize_mx(
                out=h_codes[:, cols].bitcast(FP8X4),
                scales=h_scales[:, cols],
                in_=grouped_tiles[f][:, g0 * K_PASS : g1 * K_PASS],
            )

        def multiply(f, g0, g1):
            b, q = divmod(f, STEPS_PER_BLOCK)
            if q == 0 and g0 == 0:
                acc = psum_acc.tile([P, C], F32, name="acc", tag="acc")
                acc_tiles[b] = acc
            h_codes, h_scales = code_tiles[b]
            for g in range(q * STEP_GROUPS + g0, q * STEP_GROUPS + g1):
                rows = slice(g * P, (g + 1) * P)
                nc.tensor.matmul_mx(
                    out=acc_tiles[b][:],
                    lhsT=h_codes[:, rows].bitcast(FP8X4),
                    lhsT_scale=h_scales[:, rows],
                    rhs=w_words[:, g, :].bitcast(FP4X4),
                    rhs_scale=w_planes[:, g, :],
                    start=(g == 0),
                    stop=(g == GROUPS - 1),
                )

        def sort_steps(b):
            steps = []
            state = {"src": logits[:, SLOT[b], :]}

            def compare(hi0, hi1, pick, last=False):
                def step():
                    src = state["src"]
                    if last:
                        dst = logits[:, SORTED[b], :]
                    else:
                        buf = sort_pool.tile([P, C], F32, name="buf")
                        dst = buf[:]
                    for half, op in ((0, ALU.max), (1, ALU.min)):
                        nc.vector.tensor_tensor(
                            out=pick(dst, half), in0=hi0(src), in1=hi1(src), op=op
                        )
                    state["src"] = dst

                steps.append(step)

            compare(
                lambda s: s[:, 0:HALF],
                lambda s: s[:, HALF:C],
                lambda d, half: d[:, half * HALF : (half + 1) * HALF],
            )
            compare(
                lambda s: s.rearrange("p (z o r) -> p z o r", z=2, o=2)[:, :, 0, :],
                lambda s: s.rearrange("p (z o r) -> p z o r", z=2, o=2)[:, ::-1, 1, :],
                lambda d, half: d[:, half * HALF : (half + 1) * HALF].rearrange(
                    "p (z r) -> p z r", z=2
                ),
            )
            compare(
                lambda s: s.rearrange("p (o z r) -> p o z r", o=2, z=2)[:, :, 0, :],
                lambda s: s.rearrange("p (o z r) -> p o z r", o=2, z=2)[:, :, 1, :],
                lambda d, half: d.rearrange("p (o z r) -> p o z r", o=2, z=2)[:, :, half, :],
            )
            for top in range(2, 7):
                m = 2 ** (top - 2)
                lanes = dict(q=LANES, t=2, m=m)
                compare(
                    lambda s, lanes=lanes: s.rearrange(
                        "p (q h t m) -> p h t m q", **lanes
                    )[:, :, 0, :, :],
                    lambda s, lanes=lanes: s.rearrange(
                        "p (q h t m) -> p h t m q", **lanes
                    )[:, :, 1, ::-1, ::-1],
                    lambda d, half, lanes=lanes: d.rearrange(
                        "p (h t m q) -> p h t m q", **lanes
                    )[:, :, half, :, :],
                )
                for bit in range(top - 1, 1, -1):
                    view = dict(t=2, s=2**bit)
                    compare(
                        lambda s, view=view: s.rearrange("p (h t s) -> p h t s", **view)[:, :, 0, :],
                        lambda s, view=view: s.rearrange("p (h t s) -> p h t s", **view)[:, :, 1, :],
                        lambda d, half, view=view: d.rearrange(
                            "p (h t s) -> p h t s", **view
                        )[:, :, half, :],
                    )
                compare(
                    lambda s: s.rearrange("p (r o z) -> p r o z", o=2, z=2)[:, :, 0, :],
                    lambda s: s.rearrange("p (r o z) -> p r o z", o=2, z=2)[:, :, 1, :],
                    lambda d, half: d[:, half * HALF : (half + 1) * HALF].rearrange(
                        "p (r z) -> p r z", z=2
                    ),
                )
                if top < 6:
                    compare(
                        lambda s: s.rearrange("p (o r z) -> p o z r", o=2, z=2)[:, :, 0, :],
                        lambda s: s.rearrange("p (o r z) -> p o z r", o=2, z=2)[:, :, 1, :],
                        lambda d, half: d.rearrange("p (o z r) -> p o z r", o=2, z=2)[:, :, half, :],
                    )
                else:
                    compare(
                        lambda s: s.rearrange("p (o r z) -> p z r o", o=2, z=2)[:, 0, :, :],
                        lambda s: s.rearrange("p (o r z) -> p z r o", o=2, z=2)[:, 1, :, :],
                        lambda d, half: d.rearrange("p (r o z) -> p z r o", o=2, z=2)[:, half, :, :],
                        last=True,
                    )
            return steps

        def head_logits(b):
            nc.vector.tensor_tensor(
                out=logits[:, SLOT[b], :], in0=acc_tiles[b][:], in1=b3_all[:], op=ALU.add
            )

        def head_abs(s):
            nc.vector.scalar_tensor_tensor(
                out=abs_z[:, s, :], in0=logits[:, s, :], scalar=-1.0, in1=logits[:, s, :],
                op0=ALU.mult, op1=ALU.max,
            )

        def head_sigmoid(s0, s1):
            nc.scalar.activation(out=abs_z[:, s0:s1, :], in_=abs_z[:, s0:s1, :], func=ACT.Sigmoid)

        def head(s0, s1, pairs, copies_between=0):
            order = list(pairs) + [s for s in range(s0, s1) if s not in pairs]
            for s in order:
                nc.scalar.activation(out=ln_sig[:, s, :], in_=abs_z[:, s, :], func=ACT.Ln)
            for n in range(block_banks + early_banks, block_banks + early_banks + copies_between):
                copy_bank(n, "scalar")
            for s in order:
                nc.vector.scalar_tensor_tensor(
                    out=evidence[:, s, :], in0=logits[:, s, :], scalar=0.0, in1=ln_sig[:, s, :],
                    op0=ALU.max, op1=ALU.subtract, accum_out=sum_e[:, s : s + 1],
                )
            for s in pairs:
                one = slice(s, s + 1)
                nc.vector.tensor_scalar(
                    out=c_eps[:, one], in0=sum_e[:, one], scalar1=float(C), scalar2=EPS_B,
                    op0=ALU.add, op1=ALU.mult,
                )
                copies = 1 if s in SORTED.values() else 2
                nc.scalar.activation(
                    out=ln_e2[:, s, :copies, :],
                    in_=evidence[:, one, :].to_broadcast([P, copies, C]),
                    func=ACT.Ln,
                    bias=TINY,
                )
            for s in pairs:
                one = slice(s, s + 1)
                nc.scalar.activation(
                    out=ln_ec[:, s, :], in_=evidence[:, s, :], func=ACT.Ln, bias=c_eps[:, one]
                )
                nc.vector.tensor_scalar_mul(
                    out=neg_ln_ec[:, s, :], in0=ln_ec[:, s, :], scalar1=-1.0
                )
            some = slice(s0, s1)
            nc.vector.tensor_scalar_add(out=strength[:, some], in0=sum_e[:, some], scalar1=float(C))
            nc.vector.reciprocal(out=inv_s[:, some], in_=strength[:, some])
            for s in pairs:
                one = slice(s, s + 1)
                nc.vector.tensor_scalar_mul(
                    out=belief[:, s, :], in0=evidence[:, s, :], scalar1=inv_s[:, one]
                )
                nc.vector.tensor_scalar(
                    out=belief_h2[:, s, :, :],
                    in0=evidence[:, one, :].to_broadcast([P, 2, C]),
                    scalar1=inv_s[:, one], scalar2=EPS_B / 2, op0=ALU.mult, op1=ALU.add,
                )
                nc.vector.tensor_tensor(
                    out=cap[:, s, :], in0=belief[:, s, :], in1=belief_h2[:, s, 0, :], op=ALU.mult
                )

        def head_outputs(b):
            s = SLOT[b]
            one = slice(s, s + 1)
            nc.vector.tensor_scalar_add(out=alpha[:, b, :], in0=evidence[:, s, :], scalar1=1.0)
            nc.vector.tensor_scalar_mul(out=prob[:, b, :], in0=alpha[:, b, :], scalar1=inv_s[:, one])
            nc.vector.tensor_scalar_mul(
                out=per_row[:, b : b + 1], in0=inv_s[:, one], scalar1=float(C)
            )

        def run_length(c):
            return HALF if c * CHUNK_I < HALF else HALF - 1

        def ratio(b, i):
            c, ii = divmod(i, CHUNK_I)
            n = run_length(c)
            if ii == 0:
                ratios = ratio_pool.tile([P, CHUNK_I * HALF], F32, name="ratios", tag="ratios")
                ratio_tiles[b, c] = ratios
            nc.scalar.activation(
                out=ratio_tiles[b, c][:, ii * n : (ii + 1) * n],
                in_=ln_e2[:, SLOT[b], :, :].rearrange("p d c -> p (d c)")[:, i + 1 : i + 1 + n],
                func=ACT.Sigmoid,
                bias=neg_ln_ec[:, SLOT[b], i : i + 1],
            )

        def differences(b, c):
            n = run_length(c)
            ratio_tile = ratio_pool.tile([P, CHUNK_I * HALF], F32, name="ratios", tag="ratios")
            ratio_tiles[b, c] = ratio_tile
            logs = ln_e2[:, SLOT[b], :, :].rearrange("p d c -> p (d c)")
            for ii in range(CHUNK_I):
                i = c * CHUNK_I + ii
                nc.vector.tensor_scalar_add(
                    out=ratio_tile[:, ii * n : (ii + 1) * n],
                    in0=logs[:, i + 1 : i + 1 + n],
                    scalar1=neg_ln_ec[:, SLOT[b], i : i + 1],
                )

        def long_ratio(b, c):
            for k in range(LONG_PARTS):
                width = CHUNK_I * run_length(c) // LONG_PARTS
                used = ratio_tiles[b, c][:, k * width : (k + 1) * width]
                nc.scalar.activation(out=used, in_=used, func=ACT.Sigmoid)

        def weights(b, i0, i1):
            partners = belief_h2[:, SLOT[b], :, :].rearrange("p d c -> p (d c)")
            for i in range(i0, i1):
                c, ii = divmod(i, CHUNK_I)
                n = run_length(c)
                if ii == 0:
                    weight = weight_pool.tile([P, CHUNK_I * HALF], F32, name="weight")
                    weight_tiles[b, c] = weight
                nc.vector.tensor_scalar(
                    out=weight_tiles[b, c][:, ii * n : (ii + 1) * n],
                    in0=partners[:, i + 1 : i + 1 + n],
                    scalar1=belief[:, SLOT[b], i : i + 1],
                    scalar2=cap[:, SLOT[b], i : i + 1],
                    op0=ALU.mult,
                    op1=ALU.min,
                )

        def sum_chunk(b, c):
            weight = weight_tiles[b, c]
            parts = SUM_PARTS if b == 0 else LAST_PARTS if (b, c) == (3, CHUNKS - 1) else 1
            width = CHUNK_I * run_length(c) // parts
            for k in range(parts):
                used = slice(k * width, (k + 1) * width)
                at = c * SUM_PARTS + k
                nc.vector.scalar_tensor_tensor(
                    out=weight[:, used], in0=weight[:, used], scalar=2.0,
                    in1=ratio_tiles[b, c][:, used],
                    op0=ALU.mult, op1=ALU.mult, accum_out=part[:, b, at : at + 1],
                )

        def sorted_row(i):
            if i < FIRST_RANKS:
                row = first_rows[:, i, i + 1 : C]
            else:
                k, r = divmod(i - FIRST_RANKS, ROWS_OF_PASS)
                if (i - FIRST_RANKS) % ROWS_OF_TILE == 0:
                    row_tile = h_pool.tile([P, ROWS_OF_TILE, C], F32, name="row_tile", tag="h_chunk")
                    rows["tile"] = row_tile
                at = (i - FIRST_RANKS) % ROWS_OF_TILE
                if r == 0:
                    nc.gpsimd.memset(
                        rows["tile"][:, at : at + ROWS_OF_PASS, i + 1 : i + ROWS_OF_PASS], 0.0
                    )
                row = rows["tile"][:, at, i + 1 : C]
            if i + 1 < C:
                nc.scalar.activation(
                    out=row,
                    in_=ln_ec[:, SORTED[1], i + 1 : C],
                    func=ACT.Sigmoid,
                    scale=-1.0,
                    bias=ln_e2[:, SORTED[1], 0, i : i + 1],
                )
            if i == FIRST_RANKS:
                above_acc = psum_acc.tile([P, ROWS_OF_PASS, C], F32, name="above_acc", tag="acc")
                rows["acc"] = above_acc
            if i >= FIRST_RANKS and r == ROWS_OF_PASS - 1:
                first = i - r
                nc.tensor.matmul(
                    rows["acc"][:, :, first + 1 : C],
                    lhsT=ident[:],
                    rhs=rows["tile"][:, at - r : at + 1, first + 1 : C],
                    start=(first == FIRST_RANKS),
                    stop=(first == C - 1 - ROWS_OF_PASS),
                )

        def sum_first_rows():
            nc.vector.tensor_reduce(
                out=above[:, 0, :], in_=first_rows[:].rearrange("p i j -> p j i"), axis=AX.X,
                op=ALU.add,
            )

        def sorted_dissonance():
            n = FIRST_RANKS + 1
            nc.vector.tensor_reduce(
                out=above[:, 1, n:C], in_=rows["acc"][:, :, n:C].rearrange("p r j -> p j r"),
                axis=AX.X, op=ALU.add,
            )
            nc.vector.tensor_tensor(
                out=above[:, 0, n:C], in0=above[:, 0, n:C], in1=above[:, 1, n:C], op=ALU.add
            )
            nc.vector.scalar_tensor_tensor(
                out=cap[:, SORTED[1], :], in0=cap[:, SORTED[1], :], scalar=2.0, in1=above[:, 0, :],
                op0=ALU.mult, op1=ALU.mult, accum_out=part[:, 1, 0:1],
            )

        block_banks = STEPS_PER_BLOCK * STEP_BANKS
        early_banks = 0
        nc.vector.memset(w_planes[:].bitcast(I32), 0)
        make_identity(nc, ident[:])
        nc.gpsimd.memset(per_row[:], 0.0)
        nc.gpsimd.memset(first_rows[:], 0.0)
        nc.gpsimd.memset(part[:], 0.0)
        nc.gpsimd.memset(warm[:], 0.0)
        nc.scalar.activation(out=warm[:, 1:2], in_=warm[:, 0:1], func=ACT.Sigmoid)
        for f in range(STEPS_PER_BLOCK):
            load_chunk(f)
        load_weights()
        for f in range(STEPS_PER_BLOCK, H_BUFS):
            load_chunk(f)
        for n in range(BANKS_AHEAD):
            transpose_bank(n)

        block_banks = STEPS_PER_BLOCK * STEP_BANKS
        for f in range(STEPS_PER_BLOCK):
            for j in range(STEP_BANKS):
                copy_bank(f * STEP_BANKS + j, "vector" if j == 0 else "scalar", block_banks)
            quantise(f, 0, STEP_GROUPS)
            if f == STEPS_PER_BLOCK - 2:
                for early in range(f):
                    multiply(early, 0, STEP_GROUPS)
            if f >= STEPS_PER_BLOCK - 2:
                multiply(f, 0, STEP_GROUPS)
        for n in range(block_banks, block_banks + BANKS_AHEAD):
            transpose_bank(n)

        def logits_done(b):
            head_logits(b)
            head_abs(SLOT[b])
            if b in SORTED:
                for step in sort_steps(b):
                    step()
                head_abs(SORTED[b])

        early_banks = 0
        logits_done(0)
        head_sigmoid(0, 1)
        head(0, 1, (0,), HEAD_COPIES)
        early_banks += HEAD_COPIES

        ratios_done = 0
        for f in range(STEPS_PER_BLOCK, STEPS):
            for jb in range(STEP_BANKS):
                by_vector = jb in VECTOR_BANKS[f]
                n = f * STEP_BANKS + jb
                if n < block_banks + early_banks:
                    by_vector = True
                else:
                    copy_bank(n, "vector" if by_vector else "scalar")
                if not by_vector:
                    more = min(ratios_done + RATIOS_PER_COPY, RATIOS_BESIDE)
                    for i in range(ratios_done, more):
                        ratio(0, i)
                    ratios_done = more
                if jb == 1 and f > STEPS_PER_BLOCK:
                    for g0 in range(0, STEP_GROUPS, QUANTISE_GROUPS):
                        quantise(f - 1, g0, g0 + QUANTISE_GROUPS)
                    multiply(f - 1, 0, STEP_GROUPS)
                    b, q = divmod(f - 1, STEPS_PER_BLOCK)
                    if q == STEPS_PER_BLOCK - 1:
                        logits_done(b)
        for g0 in (0, STEP_GROUPS // 2):
            quantise(STEPS - 1, g0, g0 + STEP_GROUPS // 2)
            multiply(STEPS - 1, g0, g0 + STEP_GROUPS // 2)
        logits_done(BLOCKS - 1)
        head_sigmoid(1, 3)
        for i in range(ratios_done, C):
            ratio(0, i)

        head_sigmoid(3, SLOTS)
        head(1, SLOTS, (2, 4, 3))
        for c in range(CHUNKS):
            weights(0, c * CHUNK_I, (c + 1) * CHUNK_I)
            sum_chunk(0, c)
        for b in range(BLOCKS):
            head_outputs(b)
        nc.sync.dma_start(out=out_0.rearrange("(b p) c -> p b c", p=P), in_=alpha[:])
        nc.sync.dma_start(
            out=out_1.rearrange("(b p) c -> p b c", p=P), in_=evidence[:, :BLOCKS, :]
        )
        nc.sync.dma_start(out=out_2.rearrange("(b p) c -> p b c", p=P), in_=prob[:])

        later = FIRST_RANKS + ROWS_OF_TILE * TILES_BEFORE
        row_order = list(range(FIRST_RANKS, later)) + list(range(FIRST_RANKS))
        row_order += list(range(later, C - 1))
        done = 0
        for k in range(2 * CHUNKS):
            b, c = divmod(k, CHUNKS)
            if k + DIFF_LEAD in DIFF_CHUNKS:
                b1, c1 = divmod(k + DIFF_LEAD, CHUNKS)
                differences(2 + b1, c1)
            if k in DIFF_CHUNKS:
                long_ratio(2 + b, c)
            else:
                for i in range(c * CHUNK_I, (c + 1) * CHUNK_I):
                    ratio(2 + b, i)
            more = min(C - 1, (C - 1) * (k + 1) // ROW_CHUNKS)
            for i in row_order[done:more]:
                sorted_row(i)
                if i == FIRST_RANKS - 1:
                    sum_first_rows()
            done = more
            weights(2 + b, c * CHUNK_I, (c + 1) * CHUNK_I)
            sum_chunk(2 + b, c)
        sorted_dissonance()

        nc.vector.tensor_reduce(
            out=per_row[:, BLOCKS : 2 * BLOCKS], in_=part[:], axis=AX.X, op=ALU.add
        )
        turned = psum_t.tile([P, P], F32, name="turned", tag="xt")
        nc.tensor.transpose(turned[:], per_row[:], ident[:])
        nc.vector.tensor_copy(out=per_row_t[:], in_=turned[:])
        nc.sync.dma_start(out=out_3.rearrange("(b p) -> b p", p=P), in_=per_row_t[0:BLOCKS, :])
        nc.sync.dma_start(
            out=out_4.rearrange("(b p) -> b p", p=P), in_=per_row_t[BLOCKS : 2 * BLOCKS, :]
        )
